import numpy as np
import ml_dtypes


def mxq(x, axis, fmt="e4m3"):
    dtype, down = {"e4m3": (ml_dtypes.float8_e4m3fn, 7), "e5m2": (ml_dtypes.float8_e5m2, 14)}[fmt]
    v = np.moveaxis(np.asarray(x, np.float32).astype(ml_dtypes.bfloat16).astype(np.float64), axis, -1)
    blocks = v.reshape(v.shape[:-1] + (-1, 32))
    amax = np.abs(blocks).max(-1, keepdims=True)
    byte = np.maximum(np.where(amax > 0, np.frexp(amax)[1] - 1 + 127, 0) - down, 1)
    scale = np.exp2(byte - 127.0)
    codes = (blocks / scale).astype(np.float32).astype(dtype).astype(np.float64)
    return np.moveaxis((codes * scale).reshape(v.shape), -1, axis)


WIDE = False


def mx_kscale(k):
    if not WIDE:
        return np.ones(k)
    levels = np.array([10, -10, 5, -5, 0])
    a = np.random.permutation(np.resize(levels, k // 512 * 4)).reshape(k // 512, 4)
    idx = np.arange(k)
    return np.exp2(a[idx // 512, idx % 128 // 32])


BF16 = ml_dtypes.bfloat16


def bf(x):
    return np.asarray(x, np.float32).astype(BF16)


def f64(x):
    return np.asarray(x).astype(np.float64)


E2M1 = np.array([0.0, 0.5, 1.0, 1.5, 2.0, 3.0, 4.0, 6.0, -0.0, -0.5, -1.0, -1.5, -2.0, -3.0, -4.0, -6.0])


def pack_weight(w, fmt):
    k, n = w.shape
    w = f64(bf(w)).reshape(k // 32, 32, n)
    amax = np.abs(w).max(1)
    if fmt == "e4m3":
        byte = np.frexp(amax)[1] - 1 + 127 - 7
    else:
        mant, ex = np.frexp(amax / 6.0)
        byte = np.where(mant > 0.5, ex, ex - 1) + 127
    byte = np.clip(np.where(amax > 0, byte, 1), 1, 254)
    scaled = (w * np.exp2(127.0 - byte)[:, None, :]).reshape(k, n).astype(np.float32)
    by_word = np.ascontiguousarray(scaled.reshape(k // 512, 128, 4, n).transpose(0, 1, 3, 2))
    if fmt == "e4m3":
        words = by_word.astype(ml_dtypes.float8_e4m3fn).view(np.uint8)
    else:
        c = by_word.astype(ml_dtypes.float4_e2m1fn).view(np.uint8) & 0xF
        words = c[..., 0::2] | (c[..., 1::2] << 4)
    return np.ascontiguousarray(words), np.ascontiguousarray(byte.astype(np.uint8).reshape(k // 512, 16, n))


def unpack_weight(words, scales, fmt):
    g, p, n, _ = words.shape
    if fmt == "e4m3":
        vals = np.ascontiguousarray(words).view(ml_dtypes.float8_e4m3fn).astype(np.float64)
    else:
        nib = np.empty((g, p, n, 4), np.uint8)
        nib[..., 0::2] = words & 0xF
        nib[..., 1::2] = words >> 4
        vals = E2M1[nib]
    vals = vals * np.repeat(np.exp2(scales.astype(np.float64) - 127.0), 8, axis=1)[..., None]
    return vals.transpose(0, 1, 3, 2).reshape(g * 512, n)


B, N, DIM, HEADS, MID = 4, 128, 1024, 8, 512
FMT = "e4m3"


def conprefix(xq, dw, db, uw, ub):
    h = np.tanh((xq @ dw) + f64(db))
    kv = (mxq(h, 2, "e4m3") @ uw) + f64(ub)
    return np.concatenate([np.zeros((B, N, DIM)), kv], axis=-1)


def setup_inputs():
    s = mx_kscale(DIM)
    a, m = 1.0 / np.sqrt(DIM), 1.0 / np.sqrt(MID)
    x = bf(np.random.standard_normal((B, N, DIM)) * s)
    Wqkv_words, Wqkv_scales = pack_weight((np.random.standard_normal((3 * DIM, DIM)) * a / s).T, FMT)
    down_w_words, down_w_scales = pack_weight((np.random.standard_normal((MID, DIM)) * a / s).T, FMT)
    down_b = bf(np.random.standard_normal(MID) * 0.3)
    up_w_words, up_w_scales = pack_weight((np.random.standard_normal((2 * DIM, MID)) * m).T, FMT)
    up_b = bf(np.random.standard_normal(2 * DIM) * 0.3)
    pdown_w_words, pdown_w_scales = pack_weight((np.random.standard_normal((MID, DIM)) * a / s).T, FMT)
    pdown_b = bf(np.random.standard_normal(MID) * 0.3)
    pup_w_words, pup_w_scales = pack_weight((np.random.standard_normal((2 * DIM, MID)) * m).T, FMT)
    pup_b = bf(np.random.standard_normal(2 * DIM) * 0.3)
    return {
        "x": x,
        "Wqkv_words": Wqkv_words,
        "Wqkv_scales": Wqkv_scales,
        "down_w_words": down_w_words,
        "down_w_scales": down_w_scales,
        "down_b": down_b,
        "up_w_words": up_w_words,
        "up_w_scales": up_w_scales,
        "up_b": up_b,
        "pdown_w_words": pdown_w_words,
        "pdown_w_scales": pdown_w_scales,
        "pdown_b": pdown_b,
        "pup_w_words": pup_w_words,
        "pup_w_scales": pup_w_scales,
        "pup_b": pup_b,
    }


def reference(x, Wqkv_words, Wqkv_scales, down_w_words, down_w_scales, down_b, up_w_words, up_w_scales, up_b,
              pdown_w_words, pdown_w_scales, pdown_b, pup_w_words, pup_w_scales, pup_b):
    xq = mxq(f64(x), 2, "e4m3")
    qkv = xq @ unpack_weight(Wqkv_words, Wqkv_scales, FMT)
    return (qkv + conprefix(xq, unpack_weight(pdown_w_words, pdown_w_scales, FMT), pdown_b,
                            unpack_weight(pup_w_words, pup_w_scales, FMT), pup_b)
                + conprefix(xq, unpack_weight(down_w_words, down_w_scales, FMT), down_b,
                            unpack_weight(up_w_words, up_w_scales, FMT), up_b))

@@ -1,0 +1,297 @@
+from contextlib import ExitStack
+
+import concourse.mybir as mybir
+from concourse.masks import make_identity
+
+F32 = mybir.dt.float32
+BF16 = mybir.dt.bfloat16
+I32 = mybir.dt.int32
+U32 = mybir.dt.uint32
+U8 = mybir.dt.uint8
+FP8X4 = mybir.dt.float8_e4m3fn_x4
+ADD = mybir.AluOpType.add
+TANH = mybir.ActivationFunctionType.Tanh
+
+P = 128
+PACK = 4
+PAIRS = 2
+K_PASS = P * PACK
+N_TILE = 512
+TOKEN_TILES = 4
+DIM = 1024
+MID = 512
+X_PASSES = DIM // K_PASS
+ADAPTERS = 2
+Q_CHUNKS = DIM // N_TILE
+KV_CHUNKS = 2 * DIM // N_TILE
+QUADRANTS = 4
+ROWS = 4
+
+WQKV_ROW = (0, 4)
+ADAPTER_ROW = (8, 12)
+UP_COLS = 2 * DIM
+PLANE_COLS = 3 * DIM
+
+FLOPS = 2 * TOKEN_TILES * P * (DIM * 3 * DIM + ADAPTERS * (DIM * MID + MID * 2 * DIM))
+
+
+def by_pair(ap):
+    return ap.rearrange("r (p u e) -> r u p e", u=PAIRS, e=2)
+
+
+def pair_planes(ap):
+    return ap.rearrange("r (u p e) -> r u p e", u=PAIRS, e=2)
+
+
+def tile_attention_pa_kernel(
+    tc,
+    x,
+    Wqkv_words,
+    Wqkv_scales,
+    down_w_words,
+    down_w_scales,
+    down_b,
+    up_w_words,
+    up_w_scales,
+    up_b,
+    pdown_w_words,
+    pdown_w_scales,
+    pdown_b,
+    pup_w_words,
+    pup_w_scales,
+    pup_b,
+    out,
+):
+    nc = tc.nc
+    down_words_in = (pdown_w_words, down_w_words)
+    down_scales_in = (pdown_w_scales, down_w_scales)
+    down_bias_in = (pdown_b, down_b)
+    up_words_in = (pup_w_words, up_w_words)
+    up_scales_in = (pup_w_scales, up_w_scales)
+    up_bias_in = (pup_b, up_b)
+
+    with ExitStack() as ctx:
+        ctx.enter_context(tc.manual_schedule())
+        keep = ctx.enter_context(tc.tile_pool(name="keep", bufs=1))
+        work = ctx.enter_context(tc.tile_pool(name="work", bufs=3))
+        stage = ctx.enter_context(tc.tile_pool(name="stage", bufs=8))
+        psum = ctx.enter_context(tc.psum_pool(name="psum", bufs=8))
+
+        warm = keep.tile([P, 2], F32)
+        nc.vector.memset(warm[:], 0.0)
+        nc.scalar.activation(out=warm[:, 1:2], in_=warm[:, 0:1], func=TANH)
+
+        planes = keep.tile([P, PLANE_COLS], U8, align_bytes=64)
+        bias_rows = keep.tile([P, PLANE_COLS], BF16)
+        nc.vector.memset(planes[:, UP_COLS:].bitcast(I32), 0)
+        nc.vector.memset(bias_rows[:, UP_COLS:].bitcast(I32), 0)
+        nc.vector.memset(planes[:, :UP_COLS].bitcast(I32), 0)
+        nc.vector.memset(bias_rows[:, :UP_COLS].bitcast(I32), 0)
+
+        ident = keep.tile([P, P], F32)
+        make_identity(nc, ident[:])
+        ones = keep.tile([P, P], BF16)
+        nc.gpsimd.memset(ones[:], 1.0)
+        for a in range(ADAPTERS):
+            nc.gpsimd.dma_start(
+                out=bias_rows[0:1, UP_COLS + a * MID : UP_COLS + (a + 1) * MID],
+                in_=down_bias_in[a].unsqueeze(0),
+            )
+        for a in range(ADAPTERS):
+            nc.gpsimd.dma_start(out=bias_rows[a : a + 1, :UP_COLS], in_=up_bias_in[a].unsqueeze(0))
+
+        x_sb = []
+        for i in range(TOKEN_TILES):
+            x_tile = keep.tile([P, DIM], BF16, name="x%d" % i)
+            nc.sync.dma_start(out=x_tile[:], in_=x[i])
+            x_sb.append(x_tile)
+
+        down_words = []
+        for a in range(ADAPTERS):
+            for quad in range(QUADRANTS):
+                first = 32 * quad + ADAPTER_ROW[a]
+                nc.sync.dma_start(
+                    out=planes[first : first + ROWS, UP_COLS:]
+                    .bitcast(I32)
+                    .rearrange("r (g n) -> r g n", g=X_PASSES),
+                    in_=down_scales_in[a][:, ROWS * quad : ROWS * (quad + 1), :]
+                    .bitcast(I32)
+                    .rearrange("g r n -> r g n"),
+                )
+            words = keep.tile([P, X_PASSES, MID], U32, name="down_words%d" % a, align_bytes=64)
+            nc.sync.dma_start(
+                out=words[:].bitcast(I32),
+                in_=down_words_in[a].rearrange("g p n t -> p g (n t)").bitcast(I32),
+            )
+            down_words.append(words)
+
+        wqkv = keep.tile([P, X_PASSES, 3 * DIM], U32, align_bytes=64)
+        wqkv_in = Wqkv_words.rearrange("g p n t -> p g (n t)").bitcast(I32)
+
+        def load_wqkv_chunk(chunk):
+            cols = slice(chunk * N_TILE, (chunk + 1) * N_TILE)
+            nc.sync.dma_start(out=wqkv[:, :, cols].bitcast(I32), in_=wqkv_in[:, :, cols])
+
+        for quad in range(QUADRANTS):
+            nc.sync.dma_start(
+                out=planes[32 * quad : 32 * quad + X_PASSES * ROWS, :].bitcast(I32),
+                in_=Wqkv_scales[:, ROWS * quad : ROWS * (quad + 1), :].bitcast(I32),
+            )
+        for chunk in range(Q_CHUNKS):
+            load_wqkv_chunk(chunk)
+
+        up_words = []
+        for a in range(ADAPTERS):
+            for quad in range(QUADRANTS):
+                first = 32 * quad + ADAPTER_ROW[a]
+                nc.sync.dma_start(
+                    out=planes[first : first + ROWS, :UP_COLS].bitcast(I32),
+                    in_=up_scales_in[a][0, ROWS * quad : ROWS * (quad + 1), :].bitcast(I32),
+                )
+            words = keep.tile([P, UP_COLS], U32, name="up_words%d" % a, align_bytes=64)
+            up_words.append(words)
+        for chunk in range(KV_CHUNKS):
+            cols = slice(chunk * N_TILE, (chunk + 1) * N_TILE)
+            load_wqkv_chunk(Q_CHUNKS + chunk)
+            for a in range(ADAPTERS):
+                nc.sync.dma_start(
+                    out=up_words[a][:, cols].bitcast(I32),
+                    in_=up_words_in[a].rearrange("g p n t -> p (g n t)").bitcast(I32)[:, cols],
+                )
+
+        def quantise_token_tile(sources, label):
+            flipped = psum.tile([P, 2, PAIRS, P], F32, tag="bank")
+            for s in range(2):
+                for u in range(PAIRS):
+                    nc.tensor.transpose(flipped[:, s, u, :], sources[s][u], ident[:])
+            grouped = work.tile([P, 2, P, PACK], BF16, tag="grouped", align_bytes=64)
+            nc.scalar.copy(
+                out=grouped[:].bitcast(F32), in_=flipped[:].rearrange("p s u r -> p s r u")
+            )
+            codes = keep.tile([P, 2, P], U32, name="codes_" + label, align_bytes=64)
+            scales = keep.tile([P, 2, P], U8, name="scales_" + label, align_bytes=64)
+            nc.vector.quantize_mx(
+                out=codes[:].rearrange("p s r -> p (s r)").bitcast(FP8X4),
+                scales=scales[:].rearrange("p s r -> p (s r)"),
+                in_=grouped[:].rearrange("p s r t -> p (s r t)"),
+            )
+            return codes, scales
+
+        def mx_pass(acc, tokens, s, words, plane, start, stop):
+            codes, scales = tokens
+            nc.tensor.matmul_mx(
+                out=acc[:],
+                lhsT=codes[:, s, :].bitcast(FP8X4),
+                lhsT_scale=scales[:, s, :],
+                rhs=words.bitcast(FP8X4),
+                rhs_scale=plane,
+                start=start,
+                stop=stop,
+            )
+
+        def base_passes(acc, i, chunk, stop):
+            cols = slice(chunk * N_TILE, (chunk + 1) * N_TILE)
+            for g in range(X_PASSES):
+                mx_pass(
+                    acc,
+                    x_mx[i],
+                    g,
+                    wqkv[:, g, cols],
+                    planes[WQKV_ROW[g] : P, cols],
+                    start=(g == 0),
+                    stop=(stop and g == X_PASSES - 1),
+                )
+
+        def spread_bias(cols):
+            spread = psum.tile([P, N_TILE], F32, tag="bank")
+            nc.tensor.matmul(out=spread[:], lhsT=ones[:], rhs=bias_rows[:, cols], start=True, stop=True)
+            return spread
+
+        x_mx = []
+        for i in range(TOKEN_TILES):
+            x_words = x_sb[i][:].bitcast(F32)
+            half = K_PASS // 2
+            sources = [
+                [x_words[:, g * half + u : (g + 1) * half : PAIRS] for u in range(PAIRS)]
+                for g in range(X_PASSES)
+            ]
+            x_mx.append(quantise_token_tile(sources, "x%d" % i))
+
+        down_bias = keep.tile([P, ADAPTERS, MID], F32)
+        for a in range(ADAPTERS):
+            spread = spread_bias(slice(UP_COLS + a * MID, UP_COLS + (a + 1) * MID))
+            nc.scalar.copy(out=pair_planes(down_bias[:, a, :]), in_=by_pair(spread[:]))
+
+        hidden = []
+        for i in range(TOKEN_TILES):
+            hidden_tile = keep.tile([P, ADAPTERS, MID], BF16, name="hidden%d" % i)
+            hidden.append(hidden_tile)
+        for a in range(ADAPTERS):
+            for i in range(TOKEN_TILES):
+                acc = psum.tile([P, N_TILE], F32, tag="bank")
+                for g in range(X_PASSES):
+                    mx_pass(
+                        acc,
+                        x_mx[i],
+                        g,
+                        down_words[a][:, g, :],
+                        planes[ADAPTER_ROW[a] : P, UP_COLS + g * MID : UP_COLS + (g + 1) * MID],
+                        start=(g == 0),
+                        stop=(g == X_PASSES - 1),
+                    )
+                pre = work.tile([P, MID], F32, tag="pre")
+                nc.vector.tensor_tensor(
+                    out=pair_planes(pre[:]),
+                    in0=by_pair(acc[:]),
+                    in1=pair_planes(down_bias[:, a, :]),
+                    op=ADD,
+                )
+                nc.scalar.activation(out=hidden[i][:, a, :], in_=pre[:], func=TANH)
+
+        for i in range(TOKEN_TILES):
+            for chunk in range(Q_CHUNKS):
+                acc = psum.tile([P, N_TILE], F32, tag="bank")
+                base_passes(acc, i, chunk, stop=True)
+                result = stage.tile([P, N_TILE], F32, tag="result")
+                if chunk % 2 == 0:
+                    nc.scalar.copy(out=result[:], in_=acc[:])
+                else:
+                    nc.vector.tensor_copy(out=result[:], in_=acc[:])
+                nc.sync.dma_start(out=out[i, :, chunk * N_TILE : (chunk + 1) * N_TILE], in_=result[:])
+
+        kv_bias = keep.tile([P, KV_CHUNKS, N_TILE], F32)
+
+        def make_kv_bias(chunk):
+            spread = spread_bias(slice(chunk * N_TILE, (chunk + 1) * N_TILE))
+            nc.scalar.copy(out=kv_bias[:, chunk, :], in_=spread[:])
+
+        make_kv_bias(0)
+        h_mx = []
+        for i in range(TOKEN_TILES):
+            sources = [
+                [hidden[i][:, a, :].bitcast(F32)[:, u * P : (u + 1) * P] for u in range(PAIRS)]
+                for a in range(ADAPTERS)
+            ]
+            h_mx.append(quantise_token_tile(sources, "h%d" % i))
+
+        for chunk in range(KV_CHUNKS):
+            cols = slice(chunk * N_TILE, (chunk + 1) * N_TILE)
+            if chunk + 1 < KV_CHUNKS:
+                make_kv_bias(chunk + 1)
+            for i in range(TOKEN_TILES):
+                acc = psum.tile([P, N_TILE], F32, tag="bank")
+                base_passes(acc, i, Q_CHUNKS + chunk, stop=False)
+                for a in range(ADAPTERS):
+                    mx_pass(
+                        acc,
+                        h_mx[i],
+                        a,
+                        up_words[a][:, cols],
+                        planes[ADAPTER_ROW[a] : P, cols],
+                        start=False,
+                        stop=(a == ADAPTERS - 1),
+                    )
+                result = stage.tile([P, N_TILE], F32, tag="result")
+                nc.vector.tensor_tensor(out=result[:], in0=acc[:], in1=kv_bias[:, chunk, :], op=ADD)
+                first = DIM + chunk * N_TILE
+                nc.sync.dma_start(out=out[i, :, first : first + N_TILE], in_=result[:])

@@ -133,9 +133,9 @@ def tile_attention_pa_kernel(
             nc.sync.dma_start(out=wqkv[:, :, cols].bitcast(I32), in_=wqkv_in[:, :, cols])
 
         for quad in range(QUADRANTS):
-            nc.sync.dma_start(
-                out=planes[32 * quad : 32 * quad + X_PASSES * ROWS, :].bitcast(I32),
-                in_=Wqkv_scales[:, ROWS * quad : ROWS * (quad + 1), :].bitcast(I32),
+            nc.gpsimd.dma_start(
+                out=planes[32 * quad : 32 * quad + X_PASSES * ROWS, :].bitcast(F32),
+                in_=Wqkv_scales[:, ROWS * quad : ROWS * (quad + 1), :].bitcast(F32),
             )
         for chunk in range(Q_CHUNKS):
             load_wqkv_chunk(chunk)
@@ -144,9 +144,9 @@ def tile_attention_pa_kernel(
         for a in range(ADAPTERS):
             for quad in range(QUADRANTS):
                 first = 32 * quad + ADAPTER_ROW[a]
-                nc.sync.dma_start(
-                    out=planes[first : first + ROWS, :UP_COLS].bitcast(I32),
-                    in_=up_scales_in[a][0, ROWS * quad : ROWS * (quad + 1), :].bitcast(I32),
+                nc.gpsimd.dma_start(
+                    out=planes[first : first + ROWS, :UP_COLS].bitcast(F32),
+                    in_=up_scales_in[a][0, ROWS * quad : ROWS * (quad + 1), :].bitcast(F32),
                 )
             words = keep.tile([P, UP_COLS], U32, name="up_words%d" % a, align_bytes=64)
             up_words.append(words)

@@ -27,10 +27,8 @@ KV_CHUNKS = 2 * DIM // N_TILE
 QUADRANTS = 4
 ROWS = 4
 
-WQKV_ROW = (0, 4)
-ADAPTER_ROW = (8, 12)
+DOWN_BLOCK = 2
 UP_COLS = 2 * DIM
-PLANE_COLS = 3 * DIM
 
 FLOPS = 2 * TOKEN_TILES * P * (DIM * 3 * DIM + ADAPTERS * (DIM * MID + MID * 2 * DIM))
 
@@ -74,28 +72,34 @@ def tile_attention_pa_kernel(
         ctx.enter_context(tc.manual_schedule())
         keep = ctx.enter_context(tc.tile_pool(name="keep", bufs=1))
         work = ctx.enter_context(tc.tile_pool(name="work", bufs=3))
-        stage = ctx.enter_context(tc.tile_pool(name="stage", bufs=8))
+        stage = ctx.enter_context(tc.tile_pool(name="stage", bufs=16))
         psum = ctx.enter_context(tc.psum_pool(name="psum", bufs=8))
 
+        bias_rows = keep.tile([P, UP_COLS + ADAPTERS * MID], BF16)
         warm = keep.tile([P, 2], F32)
-        nc.vector.memset(warm[:], 0.0)
-        nc.scalar.activation(out=warm[:, 1:2], in_=warm[:, 0:1], func=TANH)
-
-        planes = keep.tile([P, PLANE_COLS], U8, align_bytes=64)
-        bias_rows = keep.tile([P, PLANE_COLS], BF16)
-        nc.vector.memset(planes[:, UP_COLS:].bitcast(I32), 0)
+        adapter_planes = keep.tile([P, 3, N_TILE], U8, align_bytes=64)
+        wqkv_planes = keep.tile([P, 3 * DIM], U8, align_bytes=64)
         nc.vector.memset(bias_rows[:, UP_COLS:].bitcast(I32), 0)
-        nc.vector.memset(planes[:, :UP_COLS].bitcast(I32), 0)
+        nc.vector.memset(warm[:], 0.0)
+        nc.vector.memset(adapter_planes[:].rearrange("p b n -> p (b n)").bitcast(I32), 0)
+        nc.vector.memset(wqkv_planes[:].bitcast(I32), 0)
         nc.vector.memset(bias_rows[:, :UP_COLS].bitcast(I32), 0)
+
+        for a in range(ADAPTERS):
+            nc.scalar.dma_start(
+                out=bias_rows[0:1, UP_COLS + a * MID : UP_COLS + (a + 1) * MID],
+                in_=down_bias_in[a].unsqueeze(0),
+            )
+        nc.scalar.activation(out=warm[:, 1:2], in_=warm[:, 0:1], func=TANH)
 
         ident = keep.tile([P, P], F32)
         make_identity(nc, ident[:])
         ones = keep.tile([P, P], BF16)
         nc.gpsimd.memset(ones[:], 1.0)
-        for a in range(ADAPTERS):
+        for quad in range(QUADRANTS):
             nc.gpsimd.dma_start(
-                out=bias_rows[0:1, UP_COLS + a * MID : UP_COLS + (a + 1) * MID],
-                in_=down_bias_in[a].unsqueeze(0),
+                out=wqkv_planes[32 * quad : 32 * quad + X_PASSES * ROWS, :].bitcast(F32),
+                in_=Wqkv_scales[:, ROWS * quad : ROWS * (quad + 1), :].bitcast(F32),
             )
         for a in range(ADAPTERS):
             nc.gpsimd.dma_start(out=bias_rows[a : a + 1, :UP_COLS], in_=up_bias_in[a].unsqueeze(0))
@@ -109,14 +113,10 @@ def tile_attention_pa_kernel(
         down_words = []
         for a in range(ADAPTERS):
             for quad in range(QUADRANTS):
-                first = 32 * quad + ADAPTER_ROW[a]
+                first = 32 * quad + a * X_PASSES * ROWS
                 nc.sync.dma_start(
-                    out=planes[first : first + ROWS, UP_COLS:]
-                    .bitcast(I32)
-                    .rearrange("r (g n) -> r g n", g=X_PASSES),
-                    in_=down_scales_in[a][:, ROWS * quad : ROWS * (quad + 1), :]
-                    .bitcast(I32)
-                    .rearrange("g r n -> r g n"),
+                    out=adapter_planes[first : first + X_PASSES * ROWS, DOWN_BLOCK, :].bitcast(I32),
+                    in_=down_scales_in[a][:, ROWS * quad : ROWS * (quad + 1), :].bitcast(I32),
                 )
             words = keep.tile([P, X_PASSES, MID], U32, name="down_words%d" % a, align_bytes=64)
             nc.sync.dma_start(
@@ -132,21 +132,17 @@ def tile_attention_pa_kernel(
             cols = slice(chunk * N_TILE, (chunk + 1) * N_TILE)
             nc.sync.dma_start(out=wqkv[:, :, cols].bitcast(I32), in_=wqkv_in[:, :, cols])
 
-        for quad in range(QUADRANTS):
-            nc.gpsimd.dma_start(
-                out=planes[32 * quad : 32 * quad + X_PASSES * ROWS, :].bitcast(F32),
-                in_=Wqkv_scales[:, ROWS * quad : ROWS * (quad + 1), :].bitcast(F32),
-            )
         for chunk in range(Q_CHUNKS):
             load_wqkv_chunk(chunk)
 
         up_words = []
         for a in range(ADAPTERS):
             for quad in range(QUADRANTS):
-                first = 32 * quad + ADAPTER_ROW[a]
-                nc.gpsimd.dma_start(
-                    out=planes[first : first + ROWS, :UP_COLS].bitcast(F32),
-                    in_=up_scales_in[a][0, ROWS * quad : ROWS * (quad + 1), :].bitcast(F32),
+                nc.sync.dma_start(
+                    out=adapter_planes[32 * quad : 32 * quad + KV_CHUNKS * ROWS, a, :].bitcast(I32),
+                    in_=up_scales_in[a][0, ROWS * quad : ROWS * (quad + 1), :]
+                    .bitcast(I32)
+                    .rearrange("r (c n) -> c r n", c=KV_CHUNKS),
                 )
             words = keep.tile([P, UP_COLS], U32, name="up_words%d" % a, align_bytes=64)
             up_words.append(words)
@@ -197,7 +193,7 @@ def tile_attention_pa_kernel(
                     x_mx[i],
                     g,
                     wqkv[:, g, cols],
-                    planes[WQKV_ROW[g] : P, cols],
+                    wqkv_planes[ROWS * g : P, cols],
                     start=(g == 0),
                     stop=(stop and g == X_PASSES - 1),
                 )
@@ -235,7 +231,7 @@ def tile_attention_pa_kernel(
                         x_mx[i],
                         g,
                         down_words[a][:, g, :],
-                        planes[ADAPTER_ROW[a] : P, UP_COLS + g * MID : UP_COLS + (g + 1) * MID],
+                        adapter_planes[ROWS * (a * X_PASSES + g) : P, DOWN_BLOCK, :],
                         start=(g == 0),
                         stop=(g == X_PASSES - 1),
                     )
@@ -287,7 +283,7 @@ def tile_attention_pa_kernel(
                         h_mx[i],
                         a,
                         up_words[a][:, cols],
-                        planes[ADAPTER_ROW[a] : P, cols],
+                        adapter_planes[ROWS * chunk : P, a, :],
                         start=False,
                         stop=(a == ADAPTERS - 1),
                     )

@@ -80,10 +80,10 @@ def tile_attention_pa_kernel(
         adapter_planes = keep.tile([P, 3, N_TILE], U8, align_bytes=64)
         wqkv_planes = keep.tile([P, 3 * DIM], U8, align_bytes=64)
         nc.vector.memset(bias_rows[:, UP_COLS:].bitcast(I32), 0)
+        nc.vector.memset(bias_rows[:, :UP_COLS].bitcast(I32), 0)
         nc.vector.memset(warm[:], 0.0)
         nc.vector.memset(adapter_planes[:].rearrange("p b n -> p (b n)").bitcast(I32), 0)
         nc.vector.memset(wqkv_planes[:].bitcast(I32), 0)
-        nc.vector.memset(bias_rows[:, :UP_COLS].bitcast(I32), 0)
 
         for a in range(ADAPTERS):
             nc.scalar.dma_start(
@@ -96,13 +96,13 @@ def tile_attention_pa_kernel(
         make_identity(nc, ident[:])
         ones = keep.tile([P, P], BF16)
         nc.gpsimd.memset(ones[:], 1.0)
+        for a in range(ADAPTERS):
+            nc.gpsimd.dma_start(out=bias_rows[a : a + 1, :UP_COLS], in_=up_bias_in[a].unsqueeze(0))
         for quad in range(QUADRANTS):
             nc.gpsimd.dma_start(
                 out=wqkv_planes[32 * quad : 32 * quad + X_PASSES * ROWS, :].bitcast(F32),
                 in_=Wqkv_scales[:, ROWS * quad : ROWS * (quad + 1), :].bitcast(F32),
             )
-        for a in range(ADAPTERS):
-            nc.gpsimd.dma_start(out=bias_rows[a : a + 1, :UP_COLS], in_=up_bias_in[a].unsqueeze(0))
 
         x_sb = []
         for i in range(TOKEN_TILES):
@@ -217,6 +217,10 @@ def tile_attention_pa_kernel(
         for a in range(ADAPTERS):
             spread = spread_bias(slice(UP_COLS + a * MID, UP_COLS + (a + 1) * MID))
             nc.scalar.copy(out=pair_planes(down_bias[:, a, :]), in_=by_pair(spread[:]))
+        kv_bias = keep.tile([P, KV_CHUNKS, N_TILE], F32)
+        for chunk in range(KV_CHUNKS):
+            spread = spread_bias(slice(chunk * N_TILE, (chunk + 1) * N_TILE))
+            nc.scalar.copy(out=kv_bias[:, chunk, :], in_=spread[:])
 
         hidden = []
         for i in range(TOKEN_TILES):
@@ -255,13 +259,6 @@ def tile_attention_pa_kernel(
                     nc.vector.tensor_copy(out=result[:], in_=acc[:])
                 nc.sync.dma_start(out=out[i, :, chunk * N_TILE : (chunk + 1) * N_TILE], in_=result[:])
 
-        kv_bias = keep.tile([P, KV_CHUNKS, N_TILE], F32)
-
-        def make_kv_bias(chunk):
-            spread = spread_bias(slice(chunk * N_TILE, (chunk + 1) * N_TILE))
-            nc.scalar.copy(out=kv_bias[:, chunk, :], in_=spread[:])
-
-        make_kv_bias(0)
         h_mx = []
         for i in range(TOKEN_TILES):
             sources = [
@@ -272,8 +269,6 @@ def tile_attention_pa_kernel(
 
         for chunk in range(KV_CHUNKS):
             cols = slice(chunk * N_TILE, (chunk + 1) * N_TILE)
-            if chunk + 1 < KV_CHUNKS:
-                make_kv_bias(chunk + 1)
             for i in range(TOKEN_TILES):
                 acc = psum.tile([P, N_TILE], F32, tag="bank")
                 base_passes(acc, i, Q_CHUNKS + chunk, stop=False)

@@ -185,8 +185,8 @@ def tile_attention_pa_kernel(
                 stop=stop,
             )
 
-        def base_passes(acc, i, chunk, stop):
-            cols = slice(chunk * N_TILE, (chunk + 1) * N_TILE)
+        def base_passes(acc, i, first, width, stop):
+            cols = slice(first, first + width)
             for g in range(X_PASSES):
                 mx_pass(
                     acc,
@@ -251,7 +251,7 @@ def tile_attention_pa_kernel(
         for i in range(TOKEN_TILES):
             for chunk in range(Q_CHUNKS):
                 acc = psum.tile([P, N_TILE], F32, tag="bank")
-                base_passes(acc, i, chunk, stop=True)
+                base_passes(acc, i, chunk * N_TILE, N_TILE, stop=True)
                 result = stage.tile([P, N_TILE], F32, tag="result")
                 if chunk % 2 == 0:
                     nc.scalar.copy(out=result[:], in_=acc[:])
@@ -267,22 +267,29 @@ def tile_attention_pa_kernel(
             ]
             h_mx.append(quantise_token_tile(sources, "h%d" % i))
 
+        def kv_columns(i, chunk, offset, width):
+            first = chunk * N_TILE + offset
+            acc = psum.tile([P, width], F32, tag="bank")
+            base_passes(acc, i, DIM + first, width, stop=False)
+            for a in range(ADAPTERS):
+                mx_pass(
+                    acc,
+                    h_mx[i],
+                    a,
+                    up_words[a][:, first : first + width],
+                    adapter_planes[ROWS * chunk : P, a, offset : offset + width],
+                    start=False,
+                    stop=(a == ADAPTERS - 1),
+                )
+            result = stage.tile([P, width], F32, tag="result")
+            nc.vector.tensor_tensor(
+                out=result[:], in0=acc[:], in1=kv_bias[:, chunk, offset : offset + width], op=ADD
+            )
+            nc.sync.dma_start(out=out[i, :, DIM + first : DIM + first + width], in_=result[:])
+
         for chunk in range(KV_CHUNKS):
-            cols = slice(chunk * N_TILE, (chunk + 1) * N_TILE)
             for i in range(TOKEN_TILES):
-                acc = psum.tile([P, N_TILE], F32, tag="bank")
-                base_passes(acc, i, Q_CHUNKS + chunk, stop=False)
-                for a in range(ADAPTERS):
-                    mx_pass(
-                        acc,
-                        h_mx[i],
-                        a,
-                        up_words[a][:, cols],
-                        adapter_planes[ROWS * chunk : P, a, :],
-                        start=False,
-                        stop=(a == ADAPTERS - 1),
-                    )
-                result = stage.tile([P, N_TILE], F32, tag="result")
-                nc.vector.tensor_tensor(out=result[:], in0=acc[:], in1=kv_bias[:, chunk, :], op=ADD)
-                first = DIM + chunk * N_TILE
-                nc.sync.dma_start(out=out[i, :, first : first + N_TILE], in_=result[:])
+                last = chunk == KV_CHUNKS - 1 and i == TOKEN_TILES - 1
+                pieces = 2 if last else 1
+                for piece in range(pieces):
+                    kv_columns(i, chunk, piece * (N_TILE // pieces), N_TILE // pieces)

@@ -18,6 +18,7 @@ PAIRS = 2
 K_PASS = P * PACK
 N_TILE = 512
 TOKEN_TILES = 4
+TOKENS = TOKEN_TILES * P
 DIM = 1024
 MID = 512
 X_PASSES = DIM // K_PASS
@@ -26,19 +27,9 @@ Q_CHUNKS = DIM // N_TILE
 KV_CHUNKS = 2 * DIM // N_TILE
 QUADRANTS = 4
 ROWS = 4
-
-DOWN_BLOCK = 2
 UP_COLS = 2 * DIM
 
-FLOPS = 2 * TOKEN_TILES * P * (DIM * 3 * DIM + ADAPTERS * (DIM * MID + MID * 2 * DIM))
-
-
-def by_pair(ap):
-    return ap.rearrange("r (p u e) -> r u p e", u=PAIRS, e=2)
-
-
-def pair_planes(ap):
-    return ap.rearrange("r (u p e) -> r u p e", u=PAIRS, e=2)
+FLOPS = 2 * TOKENS * (DIM * 3 * DIM + ADAPTERS * (DIM * MID + MID * 2 * DIM))
 
 
 def tile_attention_pa_kernel(
@@ -71,37 +62,39 @@ def tile_attention_pa_kernel(
     with ExitStack() as ctx:
         ctx.enter_context(tc.manual_schedule())
         keep = ctx.enter_context(tc.tile_pool(name="keep", bufs=1))
-        work = ctx.enter_context(tc.tile_pool(name="work", bufs=3))
-        stage = ctx.enter_context(tc.tile_pool(name="stage", bufs=16))
+        work = ctx.enter_context(tc.tile_pool(name="work", bufs=4))
+        stage = ctx.enter_context(tc.tile_pool(name="stage", bufs=24))
         psum = ctx.enter_context(tc.psum_pool(name="psum", bufs=8))
 
-        bias_rows = keep.tile([P, UP_COLS + ADAPTERS * MID], BF16)
+        bias_rows = keep.tile([P, UP_COLS], BF16)
         warm = keep.tile([P, 2], F32)
-        adapter_planes = keep.tile([P, 3, N_TILE], U8, align_bytes=64)
         wqkv_planes = keep.tile([P, 3 * DIM], U8, align_bytes=64)
-        nc.vector.memset(bias_rows[:, UP_COLS:].bitcast(I32), 0)
-        nc.vector.memset(bias_rows[:, :UP_COLS].bitcast(I32), 0)
+        up_planes = keep.tile([P, ADAPTERS, N_TILE], U8, align_bytes=64)
+        down_planes_given = keep.tile([P, MID], U8, align_bytes=64)
+        down_planes = keep.tile([P, MID], U8, align_bytes=64)
         nc.vector.memset(warm[:], 0.0)
-        nc.vector.memset(adapter_planes[:].rearrange("p b n -> p (b n)").bitcast(I32), 0)
+        nc.vector.memset(bias_rows[:].bitcast(I32), 0)
         nc.vector.memset(wqkv_planes[:].bitcast(I32), 0)
+        nc.vector.memset(down_planes_given[:].bitcast(I32), 0)
+        nc.vector.memset(up_planes[:].rearrange("p b n -> p (b n)").bitcast(I32), 0)
 
         for a in range(ADAPTERS):
-            nc.scalar.dma_start(
-                out=bias_rows[0:1, UP_COLS + a * MID : UP_COLS + (a + 1) * MID],
-                in_=down_bias_in[a].unsqueeze(0),
-            )
+            nc.scalar.dma_start(out=bias_rows[a : a + 1, :], in_=up_bias_in[a].unsqueeze(0))
+        down_bias = []
+        for a in range(ADAPTERS):
+            bias_tile = keep.tile([P, PACK], BF16, name="down_bias%d" % a)
+            nc.scalar.dma_start(out=bias_tile[:], in_=down_bias_in[a].rearrange("(p t) -> p t", t=PACK))
+            down_bias.append(bias_tile)
         nc.scalar.activation(out=warm[:, 1:2], in_=warm[:, 0:1], func=TANH)
 
         ident = keep.tile([P, P], F32)
         make_identity(nc, ident[:])
         ones = keep.tile([P, P], BF16)
         nc.gpsimd.memset(ones[:], 1.0)
-        for a in range(ADAPTERS):
-            nc.gpsimd.dma_start(out=bias_rows[a : a + 1, :UP_COLS], in_=up_bias_in[a].unsqueeze(0))
         for quad in range(QUADRANTS):
             nc.gpsimd.dma_start(
-                out=wqkv_planes[32 * quad : 32 * quad + X_PASSES * ROWS, :].bitcast(F32),
-                in_=Wqkv_scales[:, ROWS * quad : ROWS * (quad + 1), :].bitcast(F32),
+                out=wqkv_planes[32 * quad : 32 * quad + X_PASSES * ROWS, DIM:].bitcast(F32),
+                in_=Wqkv_scales[:, ROWS * quad : ROWS * (quad + 1), DIM:].bitcast(F32),
             )
 
         x_sb = []
@@ -110,20 +103,11 @@ def tile_attention_pa_kernel(
             nc.sync.dma_start(out=x_tile[:], in_=x[i])
             x_sb.append(x_tile)
 
-        down_words = []
-        for a in range(ADAPTERS):
-            for quad in range(QUADRANTS):
-                first = 32 * quad + a * X_PASSES * ROWS
-                nc.sync.dma_start(
-                    out=adapter_planes[first : first + X_PASSES * ROWS, DOWN_BLOCK, :].bitcast(I32),
-                    in_=down_scales_in[a][:, ROWS * quad : ROWS * (quad + 1), :].bitcast(I32),
-                )
-            words = keep.tile([P, X_PASSES, MID], U32, name="down_words%d" % a, align_bytes=64)
+        for quad in range(QUADRANTS):
             nc.sync.dma_start(
-                out=words[:].bitcast(I32),
-                in_=down_words_in[a].rearrange("g p n t -> p g (n t)").bitcast(I32),
+                out=wqkv_planes[32 * quad : 32 * quad + X_PASSES * ROWS, :DIM].bitcast(I32),
+                in_=Wqkv_scales[:, ROWS * quad : ROWS * (quad + 1), :DIM].bitcast(I32),
             )
-            down_words.append(words)
 
         wqkv = keep.tile([P, X_PASSES, 3 * DIM], U32, align_bytes=64)
         wqkv_in = Wqkv_words.rearrange("g p n t -> p g (n t)").bitcast(I32)
@@ -135,11 +119,27 @@ def tile_attention_pa_kernel(
         for chunk in range(Q_CHUNKS):
             load_wqkv_chunk(chunk)
 
+        down_words_given = []
+        for a in range(ADAPTERS):
+            for quad in range(QUADRANTS):
+                first = 32 * quad + a * X_PASSES * ROWS
+                nc.sync.dma_start(
+                    out=down_planes_given[first : first + X_PASSES * ROWS, :].bitcast(I32),
+                    in_=down_scales_in[a][:, ROWS * quad : ROWS * (quad + 1), :].bitcast(I32),
+                )
+        for a in range(ADAPTERS):
+            words = keep.tile([P, X_PASSES, MID], U32, name="down_words_given%d" % a, align_bytes=64)
+            nc.sync.dma_start(
+                out=words[:].bitcast(I32),
+                in_=down_words_in[a].rearrange("g p n t -> p g (n t)").bitcast(I32),
+            )
+            down_words_given.append(words)
+
         up_words = []
         for a in range(ADAPTERS):
             for quad in range(QUADRANTS):
                 nc.sync.dma_start(
-                    out=adapter_planes[32 * quad : 32 * quad + KV_CHUNKS * ROWS, a, :].bitcast(I32),
+                    out=up_planes[32 * quad : 32 * quad + KV_CHUNKS * ROWS, a, :].bitcast(I32),
                     in_=up_scales_in[a][0, ROWS * quad : ROWS * (quad + 1), :]
                     .bitcast(I32)
                     .rearrange("r (c n) -> c r n", c=KV_CHUNKS),
@@ -155,129 +155,143 @@ def tile_attention_pa_kernel(
                     in_=up_words_in[a].rearrange("g p n t -> p (g n t)").bitcast(I32)[:, cols],
                 )
 
-        def quantise_token_tile(sources, label):
-            flipped = psum.tile([P, 2, PAIRS, P], F32, tag="bank")
-            for s in range(2):
+        x_codes = keep.tile([P, X_PASSES, TOKENS], U32, align_bytes=64)
+        x_scales = keep.tile([P, X_PASSES, TOKENS], U8, align_bytes=64)
+        half = K_PASS // 2
+        for i in range(TOKEN_TILES):
+            rows = slice(i * P, (i + 1) * P)
+            x_words = x_sb[i][:].bitcast(F32)
+            flipped = psum.tile([P, X_PASSES, PAIRS, P], F32, tag="bank")
+            for g in range(X_PASSES):
                 for u in range(PAIRS):
-                    nc.tensor.transpose(flipped[:, s, u, :], sources[s][u], ident[:])
-            grouped = work.tile([P, 2, P, PACK], BF16, tag="grouped", align_bytes=64)
-            nc.scalar.copy(
-                out=grouped[:].bitcast(F32), in_=flipped[:].rearrange("p s u r -> p s r u")
-            )
-            codes = keep.tile([P, 2, P], U32, name="codes_" + label, align_bytes=64)
-            scales = keep.tile([P, 2, P], U8, name="scales_" + label, align_bytes=64)
-            nc.vector.quantize_mx(
-                out=codes[:].rearrange("p s r -> p (s r)").bitcast(FP8X4),
-                scales=scales[:].rearrange("p s r -> p (s r)"),
-                in_=grouped[:].rearrange("p s r t -> p (s r t)"),
-            )
-            return codes, scales
+                    nc.tensor.transpose(
+                        flipped[:, g, u, :], x_words[:, g * half + u : (g + 1) * half : PAIRS], ident[:]
+                    )
+            grouped = work.tile([P, X_PASSES, P, PACK], BF16, tag="grouped", align_bytes=64)
+            nc.scalar.copy(out=grouped[:].bitcast(F32), in_=flipped[:].rearrange("p g u r -> p g r u"))
+            for g in range(X_PASSES):
+                nc.vector.quantize_mx(
+                    out=x_codes[:, g, rows].bitcast(FP8X4),
+                    scales=x_scales[:, g, rows],
+                    in_=grouped[:, g, :, :].rearrange("p r t -> p (r t)"),
+                )
 
-        def mx_pass(acc, tokens, s, words, plane, start, stop):
-            codes, scales = tokens
-            nc.tensor.matmul_mx(
-                out=acc[:],
-                lhsT=codes[:, s, :].bitcast(FP8X4),
-                lhsT_scale=scales[:, s, :],
-                rhs=words.bitcast(FP8X4),
-                rhs_scale=plane,
-                start=start,
-                stop=stop,
+        kv_bias = keep.tile([P, KV_CHUNKS, N_TILE], F32)
+        for chunk in range(KV_CHUNKS):
+            spread = psum.tile([P, N_TILE], F32, tag="bank")
+            nc.tensor.matmul(
+                out=spread[:],
+                lhsT=ones[:],
+                rhs=bias_rows[:, chunk * N_TILE : (chunk + 1) * N_TILE],
+                start=True,
+                stop=True,
             )
+            nc.scalar.copy(out=kv_bias[:, chunk, :], in_=spread[:])
+
+        nc.vector.tensor_copy(
+            out=down_planes[:].rearrange("p (t m) -> p m t", t=PACK),
+            in_=down_planes_given[:].rearrange("p (m t) -> p m t", t=PACK),
+        )
+        down_words = []
+        for a in range(ADAPTERS):
+            words = keep.tile([P, X_PASSES, PACK, P], U32, name="down_words%d" % a, align_bytes=64)
+            nc.vector.tensor_copy(
+                out=words[:].bitcast(I32),
+                in_=down_words_given[a][:].bitcast(I32).rearrange("p g (m t) -> p g t m", t=PACK),
+            )
+            down_words.append(words)
 
         def base_passes(acc, i, first, width, stop):
             cols = slice(first, first + width)
+            rows = slice(i * P, (i + 1) * P)
             for g in range(X_PASSES):
-                mx_pass(
-                    acc,
-                    x_mx[i],
-                    g,
-                    wqkv[:, g, cols],
-                    wqkv_planes[ROWS * g : P, cols],
+                nc.tensor.matmul_mx(
+                    out=acc[:],
+                    lhsT=x_codes[:, g, rows].bitcast(FP8X4),
+                    lhsT_scale=x_scales[:, g, rows],
+                    rhs=wqkv[:, g, cols].bitcast(FP8X4),
+                    rhs_scale=wqkv_planes[ROWS * g : P, cols],
                     start=(g == 0),
                     stop=(stop and g == X_PASSES - 1),
                 )
 
-        def spread_bias(cols):
-            spread = psum.tile([P, N_TILE], F32, tag="bank")
-            nc.tensor.matmul(out=spread[:], lhsT=ones[:], rhs=bias_rows[:, cols], start=True, stop=True)
-            return spread
-
-        x_mx = []
-        for i in range(TOKEN_TILES):
-            x_words = x_sb[i][:].bitcast(F32)
-            half = K_PASS // 2
-            sources = [
-                [x_words[:, g * half + u : (g + 1) * half : PAIRS] for u in range(PAIRS)]
-                for g in range(X_PASSES)
-            ]
-            x_mx.append(quantise_token_tile(sources, "x%d" % i))
-
-        down_bias = keep.tile([P, ADAPTERS, MID], F32)
-        for a in range(ADAPTERS):
-            spread = spread_bias(slice(UP_COLS + a * MID, UP_COLS + (a + 1) * MID))
-            nc.scalar.copy(out=pair_planes(down_bias[:, a, :]), in_=by_pair(spread[:]))
-        kv_bias = keep.tile([P, KV_CHUNKS, N_TILE], F32)
-        for chunk in range(KV_CHUNKS):
-            spread = spread_bias(slice(chunk * N_TILE, (chunk + 1) * N_TILE))
-            nc.scalar.copy(out=kv_bias[:, chunk, :], in_=spread[:])
-
-        hidden = []
-        for i in range(TOKEN_TILES):
-            hidden_tile = keep.tile([P, ADAPTERS, MID], BF16, name="hidden%d" % i)
-            hidden.append(hidden_tile)
-        for a in range(ADAPTERS):
+        for chunk in range(Q_CHUNKS):
             for i in range(TOKEN_TILES):
-                acc = psum.tile([P, N_TILE], F32, tag="bank")
-                for g in range(X_PASSES):
-                    mx_pass(
-                        acc,
-                        x_mx[i],
-                        g,
-                        down_words[a][:, g, :],
-                        adapter_planes[ROWS * (a * X_PASSES + g) : P, DOWN_BLOCK, :],
-                        start=(g == 0),
-                        stop=(g == X_PASSES - 1),
-                    )
-                pre = work.tile([P, MID], F32, tag="pre")
-                nc.vector.tensor_tensor(
-                    out=pair_planes(pre[:]),
-                    in0=by_pair(acc[:]),
-                    in1=pair_planes(down_bias[:, a, :]),
-                    op=ADD,
-                )
-                nc.scalar.activation(out=hidden[i][:, a, :], in_=pre[:], func=TANH)
-
-        for i in range(TOKEN_TILES):
-            for chunk in range(Q_CHUNKS):
                 acc = psum.tile([P, N_TILE], F32, tag="bank")
                 base_passes(acc, i, chunk * N_TILE, N_TILE, stop=True)
                 result = stage.tile([P, N_TILE], F32, tag="result")
-                if chunk % 2 == 0:
+                if chunk == 0:
                     nc.scalar.copy(out=result[:], in_=acc[:])
                 else:
                     nc.vector.tensor_copy(out=result[:], in_=acc[:])
                 nc.sync.dma_start(out=out[i, :, chunk * N_TILE : (chunk + 1) * N_TILE], in_=result[:])
 
-        h_mx = []
-        for i in range(TOKEN_TILES):
-            sources = [
-                [hidden[i][:, a, :].bitcast(F32)[:, u * P : (u + 1) * P] for u in range(PAIRS)]
-                for a in range(ADAPTERS)
-            ]
-            h_mx.append(quantise_token_tile(sources, "h%d" % i))
+        hidden = []
+        for a in range(ADAPTERS):
+            hidden_tile = keep.tile([P, PACK, TOKENS], BF16, name="hidden%d" % a)
+            hidden.append(hidden_tile)
+            for t in range(PACK):
+                acc = psum.tile([P, TOKENS], F32, tag="bank")
+                for g in range(X_PASSES):
+                    nc.tensor.matmul_mx(
+                        out=acc[:],
+                        lhsT=down_words[a][:, g, t, :].bitcast(FP8X4),
+                        lhsT_scale=down_planes[ROWS * (a * X_PASSES + g) : P, t * P : (t + 1) * P],
+                        rhs=x_codes[:, g, :].bitcast(FP8X4),
+                        rhs_scale=x_scales[:, g, :],
+                        start=(g == 0),
+                        stop=(g == X_PASSES - 1),
+                    )
+                nc.scalar.activation(
+                    out=hidden_tile[:, t, :], in_=acc[:], func=TANH, bias=down_bias[a][:, t : t + 1]
+                )
 
-        def kv_columns(i, chunk, offset, width):
-            first = chunk * N_TILE + offset
+        h_grouped = []
+        h_codes = []
+        h_scales = []
+        for a in range(ADAPTERS):
+            grouped_tile = keep.tile([P, TOKENS, PACK], BF16, name="h_grouped%d" % a, align_bytes=64)
+            codes_tile = keep.tile([P, TOKENS], U32, name="h_codes%d" % a, align_bytes=64)
+            scales_tile = keep.tile([P, TOKENS], U8, name="h_scales%d" % a, align_bytes=64)
+            h_grouped.append(grouped_tile)
+            h_codes.append(codes_tile)
+            h_scales.append(scales_tile)
+
+        def group_hidden(a, rows):
+            nc.vector.tensor_copy(
+                out=h_grouped[a][:, rows, :], in_=hidden[a][:, :, rows].rearrange("p t r -> p r t")
+            )
+
+        def quantise_hidden(a, rows):
+            nc.vector.quantize_mx(
+                out=h_codes[a][:, rows].bitcast(FP8X4),
+                scales=h_scales[a][:, rows],
+                in_=h_grouped[a][:, rows, :].rearrange("p r t -> p (r t)"),
+            )
+
+        group_hidden(0, slice(0, TOKENS))
+        quantise_hidden(0, slice(0, TOKENS))
+        tile_rows = [slice(i * P, (i + 1) * P) for i in range(TOKEN_TILES)]
+        group_hidden(1, tile_rows[0])
+        for i in range(TOKEN_TILES):
+            if i + 1 < TOKEN_TILES:
+                group_hidden(1, tile_rows[i + 1])
+            quantise_hidden(1, tile_rows[i])
+
+        def kv_open(i, chunk, offset, width):
             acc = psum.tile([P, width], F32, tag="bank")
-            base_passes(acc, i, DIM + first, width, stop=False)
+            base_passes(acc, i, DIM + chunk * N_TILE + offset, width, stop=False)
+            return acc
+
+        def kv_close(acc, i, chunk, offset, width):
+            first = chunk * N_TILE + offset
             for a in range(ADAPTERS):
-                mx_pass(
-                    acc,
-                    h_mx[i],
-                    a,
-                    up_words[a][:, first : first + width],
-                    adapter_planes[ROWS * chunk : P, a, offset : offset + width],
+                nc.tensor.matmul_mx(
+                    out=acc[:],
+                    lhsT=h_codes[a][:, tile_rows[i]].bitcast(FP8X4),
+                    lhsT_scale=h_scales[a][:, tile_rows[i]],
+                    rhs=up_words[a][:, first : first + width].bitcast(FP8X4),
+                    rhs_scale=up_planes[ROWS * chunk : P, a, offset : offset + width],
                     start=False,
                     stop=(a == ADAPTERS - 1),
                 )
@@ -287,9 +301,13 @@ def tile_attention_pa_kernel(
             )
             nc.sync.dma_start(out=out[i, :, DIM + first : DIM + first + width], in_=result[:])
 
-        for chunk in range(KV_CHUNKS):
+        opened = [kv_open(i, 0, 0, N_TILE) for i in range(TOKEN_TILES)]
+        for i in range(TOKEN_TILES):
+            kv_close(opened[i], i, 0, 0, N_TILE)
+        for chunk in range(1, KV_CHUNKS):
             for i in range(TOKEN_TILES):
                 last = chunk == KV_CHUNKS - 1 and i == TOKEN_TILES - 1
                 pieces = 2 if last else 1
+                width = N_TILE // pieces
                 for piece in range(pieces):
-                    kv_columns(i, chunk, piece * (N_TILE // pieces), N_TILE // pieces)
+                    kv_close(kv_open(i, chunk, piece * width, width), i, chunk, piece * width, width)

@@ -196,8 +196,8 @@ def tile_attention_pa_kernel(
         for a in range(ADAPTERS):
             words = keep.tile([P, X_PASSES, PACK, P], U32, name="down_words%d" % a, align_bytes=64)
             nc.vector.tensor_copy(
-                out=words[:].bitcast(I32),
-                in_=down_words_given[a][:].bitcast(I32).rearrange("p g (m t) -> p g t m", t=PACK),
+                out=words[:].bitcast(I32).rearrange("p g t m -> p g m t"),
+                in_=down_words_given[a][:].bitcast(I32).rearrange("p g (m t) -> p g m t", t=PACK),
             )
             down_words.append(words)
 

@@ -28,6 +28,7 @@ KV_CHUNKS = 2 * DIM // N_TILE
 QUADRANTS = 4
 ROWS = 4
 UP_COLS = 2 * DIM
+WARM_UP = 4
 
 FLOPS = 2 * TOKENS * (DIM * 3 * DIM + ADAPTERS * (DIM * MID + MID * 2 * DIM))
 
@@ -80,17 +81,17 @@ def tile_attention_pa_kernel(
 
         for a in range(ADAPTERS):
             nc.scalar.dma_start(out=bias_rows[a : a + 1, :], in_=up_bias_in[a].unsqueeze(0))
+        nc.scalar.activation(out=warm[:, 1:2], in_=warm[:, 0:1], func=TANH)
+
+        ones = keep.tile([P, N_TILE], BF16)
+        nc.gpsimd.memset(ones[:], 1.0)
+        ident = keep.tile([P, P], F32)
+        make_identity(nc, ident[:])
         down_bias = []
         for a in range(ADAPTERS):
             bias_tile = keep.tile([P, PACK], BF16, name="down_bias%d" % a)
-            nc.scalar.dma_start(out=bias_tile[:], in_=down_bias_in[a].rearrange("(p t) -> p t", t=PACK))
+            nc.gpsimd.dma_start(out=bias_tile[:], in_=down_bias_in[a].rearrange("(p t) -> p t", t=PACK))
             down_bias.append(bias_tile)
-        nc.scalar.activation(out=warm[:, 1:2], in_=warm[:, 0:1], func=TANH)
-
-        ident = keep.tile([P, P], F32)
-        make_identity(nc, ident[:])
-        ones = keep.tile([P, P], BF16)
-        nc.gpsimd.memset(ones[:], 1.0)
         for quad in range(QUADRANTS):
             nc.gpsimd.dma_start(
                 out=wqkv_planes[32 * quad : 32 * quad + X_PASSES * ROWS, DIM:].bitcast(F32),
@@ -158,6 +159,10 @@ def tile_attention_pa_kernel(
         x_codes = keep.tile([P, X_PASSES, TOKENS], U32, align_bytes=64)
         x_scales = keep.tile([P, X_PASSES, TOKENS], U8, align_bytes=64)
         half = K_PASS // 2
+        idle = psum.tile([P, N_TILE], F32, tag="bank")
+        for n in range(WARM_UP):
+            nc.tensor.matmul(out=idle[:], lhsT=ones[:, :P], rhs=ones[:], start=True, stop=True)
+        spreads = []
         for i in range(TOKEN_TILES):
             rows = slice(i * P, (i + 1) * P)
             x_words = x_sb[i][:].bitcast(F32)
@@ -167,6 +172,15 @@ def tile_attention_pa_kernel(
                     nc.tensor.transpose(
                         flipped[:, g, u, :], x_words[:, g * half + u : (g + 1) * half : PAIRS], ident[:]
                     )
+            spread = psum.tile([P, N_TILE], F32, tag="bank")
+            nc.tensor.matmul(
+                out=spread[:],
+                lhsT=ones[:, :P],
+                rhs=bias_rows[:, i * N_TILE : (i + 1) * N_TILE],
+                start=True,
+                stop=True,
+            )
+            spreads.append(spread)
             grouped = work.tile([P, X_PASSES, P, PACK], BF16, tag="grouped", align_bytes=64)
             nc.scalar.copy(out=grouped[:].bitcast(F32), in_=flipped[:].rearrange("p g u r -> p g r u"))
             for g in range(X_PASSES):
@@ -178,15 +192,7 @@ def tile_attention_pa_kernel(
 
         kv_bias = keep.tile([P, KV_CHUNKS, N_TILE], F32)
         for chunk in range(KV_CHUNKS):
-            spread = psum.tile([P, N_TILE], F32, tag="bank")
-            nc.tensor.matmul(
-                out=spread[:],
-                lhsT=ones[:],
-                rhs=bias_rows[:, chunk * N_TILE : (chunk + 1) * N_TILE],
-                start=True,
-                stop=True,
-            )
-            nc.scalar.copy(out=kv_bias[:, chunk, :], in_=spread[:])
+            nc.scalar.copy(out=kv_bias[:, chunk, :], in_=spreads[chunk][:])
 
         nc.vector.tensor_copy(
             out=down_planes[:].rearrange("p (t m) -> p m t", t=PACK),

@@ -25,6 +25,8 @@ X_PASSES = DIM // K_PASS
 ADAPTERS = 2
 Q_CHUNKS = DIM // N_TILE
 KV_CHUNKS = 2 * DIM // N_TILE
+WIDE = 2 * N_TILE
+KV_HALVES = 2 * DIM // WIDE
 QUADRANTS = 4
 ROWS = 4
 UP_COLS = 2 * DIM
@@ -64,7 +66,7 @@ def tile_attention_pa_kernel(
         ctx.enter_context(tc.manual_schedule())
         keep = ctx.enter_context(tc.tile_pool(name="keep", bufs=1))
         work = ctx.enter_context(tc.tile_pool(name="work", bufs=4))
-        stage = ctx.enter_context(tc.tile_pool(name="stage", bufs=24))
+        stage = ctx.enter_context(tc.tile_pool(name="stage", bufs=12))
         psum = ctx.enter_context(tc.psum_pool(name="psum", bufs=8))
 
         bias_rows = keep.tile([P, UP_COLS], BF16)
@@ -113,12 +115,12 @@ def tile_attention_pa_kernel(
         wqkv = keep.tile([P, X_PASSES, 3 * DIM], U32, align_bytes=64)
         wqkv_in = Wqkv_words.rearrange("g p n t -> p g (n t)").bitcast(I32)
 
-        def load_wqkv_chunk(chunk):
-            cols = slice(chunk * N_TILE, (chunk + 1) * N_TILE)
+        def load_wqkv(first, width):
+            cols = slice(first, first + width)
             nc.sync.dma_start(out=wqkv[:, :, cols].bitcast(I32), in_=wqkv_in[:, :, cols])
 
         for chunk in range(Q_CHUNKS):
-            load_wqkv_chunk(chunk)
+            load_wqkv(chunk * N_TILE, N_TILE)
 
         down_words_given = []
         for a in range(ADAPTERS):
@@ -128,7 +130,6 @@ def tile_attention_pa_kernel(
                     out=down_planes_given[first : first + X_PASSES * ROWS, :].bitcast(I32),
                     in_=down_scales_in[a][:, ROWS * quad : ROWS * (quad + 1), :].bitcast(I32),
                 )
-        for a in range(ADAPTERS):
             words = keep.tile([P, X_PASSES, MID], U32, name="down_words_given%d" % a, align_bytes=64)
             nc.sync.dma_start(
                 out=words[:].bitcast(I32),
@@ -136,8 +137,7 @@ def tile_attention_pa_kernel(
             )
             down_words_given.append(words)
 
-        up_words = []
-        for a in range(ADAPTERS):
+        def load_up_planes(a):
             for quad in range(QUADRANTS):
                 nc.sync.dma_start(
                     out=up_planes[32 * quad : 32 * quad + KV_CHUNKS * ROWS, a, :].bitcast(I32),
@@ -145,16 +145,27 @@ def tile_attention_pa_kernel(
                     .bitcast(I32)
                     .rearrange("r (c n) -> c r n", c=KV_CHUNKS),
                 )
+
+        up_words = []
+        for a in range(ADAPTERS):
             words = keep.tile([P, UP_COLS], U32, name="up_words%d" % a, align_bytes=64)
             up_words.append(words)
-        for chunk in range(KV_CHUNKS):
-            cols = slice(chunk * N_TILE, (chunk + 1) * N_TILE)
-            load_wqkv_chunk(Q_CHUNKS + chunk)
-            for a in range(ADAPTERS):
-                nc.sync.dma_start(
-                    out=up_words[a][:, cols].bitcast(I32),
-                    in_=up_words_in[a].rearrange("g p n t -> p (g n t)").bitcast(I32)[:, cols],
-                )
+
+        def load_up_words(a, part):
+            cols = slice(part * WIDE, (part + 1) * WIDE)
+            nc.sync.dma_start(
+                out=up_words[a][:, cols].bitcast(I32),
+                in_=up_words_in[a].rearrange("g p n t -> p (g n t)").bitcast(I32)[:, cols],
+            )
+
+        load_up_planes(0)
+        load_wqkv(DIM, WIDE)
+        load_up_planes(1)
+        load_up_words(0, 0)
+        load_up_words(1, 0)
+        load_wqkv(DIM + WIDE, WIDE)
+        load_up_words(0, 1)
+        load_up_words(1, 1)
 
         x_codes = keep.tile([P, X_PASSES, TOKENS], U32, align_bytes=64)
         x_scales = keep.tile([P, X_PASSES, TOKENS], U8, align_bytes=64)
@@ -194,10 +205,6 @@ def tile_attention_pa_kernel(
         for chunk in range(KV_CHUNKS):
             nc.scalar.copy(out=kv_bias[:, chunk, :], in_=spreads[chunk][:])
 
-        nc.vector.tensor_copy(
-            out=down_planes[:].rearrange("p (t m) -> p m t", t=PACK),
-            in_=down_planes_given[:].rearrange("p (m t) -> p m t", t=PACK),
-        )
         down_words = []
         for a in range(ADAPTERS):
             words = keep.tile([P, X_PASSES, PACK, P], U32, name="down_words%d" % a, align_bytes=64)
@@ -206,6 +213,11 @@ def tile_attention_pa_kernel(
                 in_=down_words_given[a][:].bitcast(I32).rearrange("p g (m t) -> p g m t", t=PACK),
             )
             down_words.append(words)
+            if a == 0:
+                nc.vector.tensor_copy(
+                    out=down_planes[:].rearrange("p (t m) -> p m t", t=PACK),
+                    in_=down_planes_given[:].rearrange("p (m t) -> p m t", t=PACK),
+                )
 
         def base_passes(acc, i, first, width, stop):
             cols = slice(first, first + width)
@@ -221,16 +233,19 @@ def tile_attention_pa_kernel(
                     stop=(stop and g == X_PASSES - 1),
                 )
 
+        results = {}
         for chunk in range(Q_CHUNKS):
+            cols = slice(chunk * N_TILE, (chunk + 1) * N_TILE)
             for i in range(TOKEN_TILES):
                 acc = psum.tile([P, N_TILE], F32, tag="bank")
                 base_passes(acc, i, chunk * N_TILE, N_TILE, stop=True)
-                result = stage.tile([P, N_TILE], F32, tag="result")
                 if chunk == 0:
-                    nc.scalar.copy(out=result[:], in_=acc[:])
+                    result = stage.tile([P, WIDE], F32, tag="result")
+                    results[i] = result
+                    nc.scalar.copy(out=results[i][:, cols], in_=acc[:])
                 else:
-                    nc.vector.tensor_copy(out=result[:], in_=acc[:])
-                nc.sync.dma_start(out=out[i, :, chunk * N_TILE : (chunk + 1) * N_TILE], in_=result[:])
+                    nc.vector.tensor_copy(out=results[i][:, cols], in_=acc[:])
+                    nc.sync.dma_start(out=out[i, :, :WIDE], in_=results[i][:])
 
         hidden = []
         for a in range(ADAPTERS):
@@ -284,13 +299,28 @@ def tile_attention_pa_kernel(
                 group_hidden(1, tile_rows[i + 1])
             quantise_hidden(1, tile_rows[i])
 
-        def kv_open(i, chunk, offset, width):
+        pieces = []
+        for part in range(KV_HALVES):
+            for i in range(TOKEN_TILES):
+                last = part == KV_HALVES - 1 and i == TOKEN_TILES - 1
+                widths = [N_TILE, N_TILE // 2, N_TILE // 2] if last else [N_TILE, N_TILE]
+                first = part * WIDE
+                for width in widths:
+                    first += width
+                    whole = first == (part + 1) * WIDE
+                    stored = width if last else (WIDE if whole else 0)
+                    pieces.append((i, first - width, width, stored))
+
+        def kv_open(piece):
+            i, first, width, stored = piece
             acc = psum.tile([P, width], F32, tag="bank")
-            base_passes(acc, i, DIM + chunk * N_TILE + offset, width, stop=False)
+            base_passes(acc, i, DIM + first, width, stop=False)
             return acc
 
-        def kv_close(acc, i, chunk, offset, width):
-            first = chunk * N_TILE + offset
+        def kv_close(acc, piece):
+            i, first, width, stored = piece
+            chunk = first // N_TILE
+            offset = first % N_TILE
             for a in range(ADAPTERS):
                 nc.tensor.matmul_mx(
                     out=acc[:],
@@ -301,19 +331,26 @@ def tile_attention_pa_kernel(
                     start=False,
                     stop=(a == ADAPTERS - 1),
                 )
-            result = stage.tile([P, width], F32, tag="result")
+            if first % WIDE == 0:
+                result = stage.tile([P, WIDE], F32, tag="result")
+                results[i] = result
+            place = first % WIDE
             nc.vector.tensor_tensor(
-                out=result[:], in0=acc[:], in1=kv_bias[:, chunk, offset : offset + width], op=ADD
+                out=results[i][:, place : place + width],
+                in0=acc[:],
+                in1=kv_bias[:, chunk, offset : offset + width],
+                op=ADD,
             )
-            nc.sync.dma_start(out=out[i, :, DIM + first : DIM + first + width], in_=result[:])
+            if stored:
+                end = first + width
+                nc.sync.dma_start(
+                    out=out[i, :, DIM + end - stored : DIM + end],
+                    in_=results[i][:, place + width - stored : place + width],
+                )
 
-        opened = [kv_open(i, 0, 0, N_TILE) for i in range(TOKEN_TILES)]
-        for i in range(TOKEN_TILES):
-            kv_close(opened[i], i, 0, 0, N_TILE)
-        for chunk in range(1, KV_CHUNKS):
-            for i in range(TOKEN_TILES):
-                last = chunk == KV_CHUNKS - 1 and i == TOKEN_TILES - 1
-                pieces = 2 if last else 1
-                width = N_TILE // pieces
-                for piece in range(pieces):
-                    kv_close(kv_open(i, chunk, piece * width, width), i, chunk, piece * width, width)
+        AHEAD = 4
+        opened = [kv_open(piece) for piece in pieces[:AHEAD]]
+        for n in range(AHEAD):
+            kv_close(opened[n], pieces[n])
+        for piece in pieces[AHEAD:]:
+            kv_close(kv_open(piece), piece)

@@ -75,6 +75,8 @@ def tile_attention_pa_kernel(
         up_planes = keep.tile([P, ADAPTERS, N_TILE], U8, align_bytes=64)
         down_planes_given = keep.tile([P, MID], U8, align_bytes=64)
         down_planes = keep.tile([P, MID], U8, align_bytes=64)
+        ones = keep.tile([P, N_TILE], BF16)
+        nc.vector.memset(ones[:], 1.0)
         nc.vector.memset(warm[:], 0.0)
         nc.vector.memset(bias_rows[:].bitcast(I32), 0)
         nc.vector.memset(wqkv_planes[:].bitcast(I32), 0)
@@ -85,8 +87,6 @@ def tile_attention_pa_kernel(
             nc.scalar.dma_start(out=bias_rows[a : a + 1, :], in_=up_bias_in[a].unsqueeze(0))
         nc.scalar.activation(out=warm[:, 1:2], in_=warm[:, 0:1], func=TANH)
 
-        ones = keep.tile([P, N_TILE], BF16)
-        nc.gpsimd.memset(ones[:], 1.0)
         ident = keep.tile([P, P], F32)
         make_identity(nc, ident[:])
         down_bias = []
@@ -183,15 +183,16 @@ def tile_attention_pa_kernel(
                     nc.tensor.transpose(
                         flipped[:, g, u, :], x_words[:, g * half + u : (g + 1) * half : PAIRS], ident[:]
                     )
-            spread = psum.tile([P, N_TILE], F32, tag="bank")
-            nc.tensor.matmul(
-                out=spread[:],
-                lhsT=ones[:, :P],
-                rhs=bias_rows[:, i * N_TILE : (i + 1) * N_TILE],
-                start=True,
-                stop=True,
-            )
-            spreads.append(spread)
+            for chunk in range(i - 1, i + 1) if i % 2 == 1 else []:
+                spread = psum.tile([P, N_TILE], F32, tag="bank")
+                nc.tensor.matmul(
+                    out=spread[:],
+                    lhsT=ones[:, :P],
+                    rhs=bias_rows[:, chunk * N_TILE : (chunk + 1) * N_TILE],
+                    start=True,
+                    stop=True,
+                )
+                spreads.append(spread)
             grouped = work.tile([P, X_PASSES, P, PACK], BF16, tag="grouped", align_bytes=64)
             nc.scalar.copy(out=grouped[:].bitcast(F32), in_=flipped[:].rearrange("p g u r -> p g r u"))
             for g in range(X_PASSES):
@@ -348,7 +349,7 @@ def tile_attention_pa_kernel(
                     in_=results[i][:, place + width - stored : place + width],
                 )
 
-        AHEAD = 4
+        AHEAD = 7
         opened = [kv_open(piece) for piece in pieces[:AHEAD]]
         for n in range(AHEAD):
             kv_close(opened[n], pieces[n])

@@ -89,16 +89,6 @@ def tile_attention_pa_kernel(
 
         ident = keep.tile([P, P], F32)
         make_identity(nc, ident[:])
-        down_bias = []
-        for a in range(ADAPTERS):
-            bias_tile = keep.tile([P, PACK], BF16, name="down_bias%d" % a)
-            nc.gpsimd.dma_start(out=bias_tile[:], in_=down_bias_in[a].rearrange("(p t) -> p t", t=PACK))
-            down_bias.append(bias_tile)
-        for quad in range(QUADRANTS):
-            nc.gpsimd.dma_start(
-                out=wqkv_planes[32 * quad : 32 * quad + X_PASSES * ROWS, DIM:].bitcast(F32),
-                in_=Wqkv_scales[:, ROWS * quad : ROWS * (quad + 1), DIM:].bitcast(F32),
-            )
 
         x_sb = []
         for i in range(TOKEN_TILES):
@@ -136,6 +126,16 @@ def tile_attention_pa_kernel(
                 in_=down_words_in[a].rearrange("g p n t -> p g (n t)").bitcast(I32),
             )
             down_words_given.append(words)
+        down_bias = []
+        for a in range(ADAPTERS):
+            bias_tile = keep.tile([P, PACK], BF16, name="down_bias%d" % a)
+            nc.sync.dma_start(out=bias_tile[:], in_=down_bias_in[a].rearrange("(p t) -> p t", t=PACK))
+            down_bias.append(bias_tile)
+        for quad in range(QUADRANTS):
+            nc.sync.dma_start(
+                out=wqkv_planes[32 * quad : 32 * quad + X_PASSES * ROWS, DIM:].bitcast(I32),
+                in_=Wqkv_scales[:, ROWS * quad : ROWS * (quad + 1), DIM:].bitcast(I32),
+            )
 
         def load_up_planes(a):
             for quad in range(QUADRANTS):
@@ -158,10 +158,10 @@ def tile_attention_pa_kernel(
                 in_=up_words_in[a].rearrange("g p n t -> p (g n t)").bitcast(I32)[:, cols],
             )
 
-        load_up_planes(0)
         load_wqkv(DIM, WIDE)
-        load_up_planes(1)
+        load_up_planes(0)
         load_up_words(0, 0)
+        load_up_planes(1)
         load_up_words(1, 0)
         load_wqkv(DIM + WIDE, WIDE)
         load_up_words(0, 1)

@@ -30,7 +30,7 @@ KV_HALVES = 2 * DIM // WIDE
 QUADRANTS = 4
 ROWS = 4
 UP_COLS = 2 * DIM
-WARM_UP = 4
+WARM_UP = 6
 
 FLOPS = 2 * TOKENS * (DIM * 3 * DIM + ADAPTERS * (DIM * MID + MID * 2 * DIM))
 

@@ -30,6 +30,8 @@ KV_HALVES = 2 * DIM // WIDE
 QUADRANTS = 4
 ROWS = 4
 UP_COLS = 2 * DIM
+BLOCK = 32
+BLOCKS = UP_COLS // BLOCK
 WARM_UP = 6
 
 FLOPS = 2 * TOKENS * (DIM * 3 * DIM + ADAPTERS * (DIM * MID + MID * 2 * DIM))
@@ -69,7 +71,7 @@ def tile_attention_pa_kernel(
         stage = ctx.enter_context(tc.tile_pool(name="stage", bufs=12))
         psum = ctx.enter_context(tc.psum_pool(name="psum", bufs=8))
 
-        bias_rows = keep.tile([P, UP_COLS], BF16)
+        bias_rows = keep.tile([P, BLOCK], BF16)
         warm = keep.tile([P, 2], F32)
         wqkv_planes = keep.tile([P, 3 * DIM], U8, align_bytes=64)
         up_planes = keep.tile([P, ADAPTERS, N_TILE], U8, align_bytes=64)
@@ -78,13 +80,15 @@ def tile_attention_pa_kernel(
         ones = keep.tile([P, N_TILE], BF16)
         nc.vector.memset(ones[:], 1.0)
         nc.vector.memset(warm[:], 0.0)
-        nc.vector.memset(bias_rows[:].bitcast(I32), 0)
         nc.vector.memset(wqkv_planes[:].bitcast(I32), 0)
         nc.vector.memset(down_planes_given[:].bitcast(I32), 0)
         nc.vector.memset(up_planes[:].rearrange("p b n -> p (b n)").bitcast(I32), 0)
 
         for a in range(ADAPTERS):
-            nc.scalar.dma_start(out=bias_rows[a : a + 1, :], in_=up_bias_in[a].unsqueeze(0))
+            nc.scalar.dma_start(
+                out=bias_rows[a * BLOCKS : (a + 1) * BLOCKS, :],
+                in_=up_bias_in[a].rearrange("(b j) -> b j", j=BLOCK),
+            )
         nc.scalar.activation(out=warm[:, 1:2], in_=warm[:, 0:1], func=TANH)
 
         ident = keep.tile([P, P], F32)
@@ -173,7 +177,6 @@ def tile_attention_pa_kernel(
         idle = psum.tile([P, N_TILE], F32, tag="bank")
         for n in range(WARM_UP):
             nc.tensor.matmul(out=idle[:], lhsT=ones[:, :P], rhs=ones[:], start=True, stop=True)
-        spreads = []
         for i in range(TOKEN_TILES):
             rows = slice(i * P, (i + 1) * P)
             x_words = x_sb[i][:].bitcast(F32)
@@ -183,16 +186,9 @@ def tile_attention_pa_kernel(
                     nc.tensor.transpose(
                         flipped[:, g, u, :], x_words[:, g * half + u : (g + 1) * half : PAIRS], ident[:]
                     )
-            for chunk in range(i - 1, i + 1) if i % 2 == 1 else []:
-                spread = psum.tile([P, N_TILE], F32, tag="bank")
-                nc.tensor.matmul(
-                    out=spread[:],
-                    lhsT=ones[:, :P],
-                    rhs=bias_rows[:, chunk * N_TILE : (chunk + 1) * N_TILE],
-                    start=True,
-                    stop=True,
-                )
-                spreads.append(spread)
+            if i == TOKEN_TILES // 2 - 1:
+                for n in range(2):
+                    nc.tensor.matmul(out=idle[:], lhsT=ones[:, :P], rhs=ones[:], start=True, stop=True)
             grouped = work.tile([P, X_PASSES, P, PACK], BF16, tag="grouped", align_bytes=64)
             nc.scalar.copy(out=grouped[:].bitcast(F32), in_=flipped[:].rearrange("p g u r -> p g r u"))
             for g in range(X_PASSES):
@@ -202,9 +198,26 @@ def tile_attention_pa_kernel(
                     in_=grouped[:, g, :, :].rearrange("p r t -> p (r t)"),
                 )
 
-        kv_bias = keep.tile([P, KV_CHUNKS, N_TILE], F32)
-        for chunk in range(KV_CHUNKS):
-            nc.scalar.copy(out=kv_bias[:, chunk, :], in_=spreads[chunk][:])
+        fold = keep.tile([P, BLOCKS], BF16)
+        nc.vector.tensor_tensor(out=fold[:], in0=ident[:, :BLOCKS], in1=ident[:, BLOCKS:], op=ADD)
+        bias_cols = keep.tile([P, QUADRANTS, BLOCK], BF16)
+        nc.vector.tensor_copy(
+            out=bias_cols[:], in_=bias_rows[:].unsqueeze(1).to_broadcast([P, QUADRANTS, BLOCK])
+        )
+        bias_blocks = keep.tile([P, KV_CHUNKS, N_TILE], F32, align_bytes=64)
+        kv_bias = keep.tile([P, KV_CHUNKS, N_TILE], F32, align_bytes=64)
+        chunk_blocks = N_TILE // BLOCK
+
+        def repeat_bias(spread, chunk):
+            nc.scalar.copy(
+                out=bias_blocks[:, chunk, :].rearrange("p (b i) -> p b i", i=BLOCK),
+                in_=spread[:, chunk * chunk_blocks : (chunk + 1) * chunk_blocks]
+                .unsqueeze(2)
+                .to_broadcast([P, chunk_blocks, BLOCK]),
+            )
+
+        def turn_bias(chunk):
+            nc.vector.transpose(out=kv_bias[:, chunk, :], in_=bias_blocks[:, chunk, :])
 
         down_words = []
         for a in range(ADAPTERS):
@@ -247,6 +260,17 @@ def tile_attention_pa_kernel(
                 else:
                     nc.vector.tensor_copy(out=results[i][:, cols], in_=acc[:])
                     nc.sync.dma_start(out=out[i, :, :WIDE], in_=results[i][:])
+            if chunk == 0:
+                spread = psum.tile([P, BLOCKS], F32, tag="bank")
+                nc.tensor.matmul(
+                    out=spread[:],
+                    lhsT=bias_cols[:].rearrange("p r j -> p (r j)"),
+                    rhs=fold[:],
+                    start=True,
+                    stop=True,
+                )
+                for kv_chunk in range(KV_CHUNKS):
+                    repeat_bias(spread, kv_chunk)
 
         hidden = []
         for a in range(ADAPTERS):
@@ -299,6 +323,9 @@ def tile_attention_pa_kernel(
             if i + 1 < TOKEN_TILES:
                 group_hidden(1, tile_rows[i + 1])
             quantise_hidden(1, tile_rows[i])
+
+        for chunk in range(KV_CHUNKS // 2):
+            turn_bias(chunk)
 
         pieces = []
         for part in range(KV_HALVES):
@@ -353,5 +380,7 @@ def tile_attention_pa_kernel(
         opened = [kv_open(piece) for piece in pieces[:AHEAD]]
         for n in range(AHEAD):
             kv_close(opened[n], pieces[n])
+            if n % 2 == 1 and n < KV_CHUNKS:
+                turn_bias(KV_CHUNKS // 2 + n // 2)
         for piece in pieces[AHEAD:]:
             kv_close(kv_open(piece), piece)

@@ -75,36 +75,41 @@ def tile_attention_pa_kernel(
         warm = keep.tile([P, 2], F32)
         wqkv_planes = keep.tile([P, 3 * DIM], U8, align_bytes=64)
         up_planes = keep.tile([P, ADAPTERS, N_TILE], U8, align_bytes=64)
-        down_planes_given = keep.tile([P, MID], U8, align_bytes=64)
-        down_planes = keep.tile([P, MID], U8, align_bytes=64)
+        down_planes_given = keep.tile([P, ADAPTERS, MID], U8, align_bytes=64)
+        down_planes = keep.tile([P, ADAPTERS, MID], U8, align_bytes=64)
         ones = keep.tile([P, N_TILE], BF16)
         nc.vector.memset(ones[:], 1.0)
         nc.vector.memset(warm[:], 0.0)
         nc.vector.memset(wqkv_planes[:].bitcast(I32), 0)
-        nc.vector.memset(down_planes_given[:].bitcast(I32), 0)
+        nc.vector.memset(down_planes_given[:].rearrange("p a n -> p (a n)").bitcast(I32), 0)
         nc.vector.memset(up_planes[:].rearrange("p b n -> p (b n)").bitcast(I32), 0)
 
-        for a in range(ADAPTERS):
-            nc.scalar.dma_start(
-                out=bias_rows[a * BLOCKS : (a + 1) * BLOCKS, :],
-                in_=up_bias_in[a].rearrange("(b j) -> b j", j=BLOCK),
-            )
+        def load_up_bias():
+            for a in range(ADAPTERS):
+                nc.scalar.dma_start(
+                    out=bias_rows[a * BLOCKS : (a + 1) * BLOCKS, :],
+                    in_=up_bias_in[a].rearrange("(b j) -> b j", j=BLOCK),
+                )
+
+        load_up_bias()
         nc.scalar.activation(out=warm[:, 1:2], in_=warm[:, 0:1], func=TANH)
 
         ident = keep.tile([P, P], F32)
         make_identity(nc, ident[:])
 
         x_sb = []
-        for i in range(TOKEN_TILES):
+
+        def load_x(i):
             x_tile = keep.tile([P, DIM], BF16, name="x%d" % i)
             nc.sync.dma_start(out=x_tile[:], in_=x[i])
             x_sb.append(x_tile)
 
-        for quad in range(QUADRANTS):
-            nc.sync.dma_start(
-                out=wqkv_planes[32 * quad : 32 * quad + X_PASSES * ROWS, :DIM].bitcast(I32),
-                in_=Wqkv_scales[:, ROWS * quad : ROWS * (quad + 1), :DIM].bitcast(I32),
-            )
+        def load_wqkv_scales(first, last):
+            for quad in range(QUADRANTS):
+                nc.sync.dma_start(
+                    out=wqkv_planes[32 * quad : 32 * quad + X_PASSES * ROWS, first:last].bitcast(I32),
+                    in_=Wqkv_scales[:, ROWS * quad : ROWS * (quad + 1), first:last].bitcast(I32),
+                )
 
         wqkv = keep.tile([P, X_PASSES, 3 * DIM], U32, align_bytes=64)
         wqkv_in = Wqkv_words.rearrange("g p n t -> p g (n t)").bitcast(I32)
@@ -113,33 +118,36 @@ def tile_attention_pa_kernel(
             cols = slice(first, first + width)
             nc.sync.dma_start(out=wqkv[:, :, cols].bitcast(I32), in_=wqkv_in[:, :, cols])
 
-        for chunk in range(Q_CHUNKS):
-            load_wqkv(chunk * N_TILE, N_TILE)
+        def load_wqkv_pass(g, first, width):
+            cols = slice(first, first + width)
+            nc.sync.dma_start(out=wqkv[:, g, cols].bitcast(I32), in_=wqkv_in[:, g, cols])
 
         down_words_given = []
         for a in range(ADAPTERS):
+            words = keep.tile([P, X_PASSES, MID], U32, name="down_words_given%d" % a, align_bytes=64)
+            down_words_given.append(words)
+
+        def load_down_planes(a):
             for quad in range(QUADRANTS):
-                first = 32 * quad + a * X_PASSES * ROWS
                 nc.sync.dma_start(
-                    out=down_planes_given[first : first + X_PASSES * ROWS, :].bitcast(I32),
+                    out=down_planes_given[32 * quad : 32 * quad + X_PASSES * ROWS, a, :].bitcast(I32),
                     in_=down_scales_in[a][:, ROWS * quad : ROWS * (quad + 1), :].bitcast(I32),
                 )
-            words = keep.tile([P, X_PASSES, MID], U32, name="down_words_given%d" % a, align_bytes=64)
+
+        def load_down_words(a):
             nc.sync.dma_start(
-                out=words[:].bitcast(I32),
+                out=down_words_given[a][:].bitcast(I32),
                 in_=down_words_in[a].rearrange("g p n t -> p g (n t)").bitcast(I32),
             )
-            down_words_given.append(words)
+
         down_bias = []
         for a in range(ADAPTERS):
             bias_tile = keep.tile([P, PACK], BF16, name="down_bias%d" % a)
-            nc.sync.dma_start(out=bias_tile[:], in_=down_bias_in[a].rearrange("(p t) -> p t", t=PACK))
             down_bias.append(bias_tile)
-        for quad in range(QUADRANTS):
-            nc.sync.dma_start(
-                out=wqkv_planes[32 * quad : 32 * quad + X_PASSES * ROWS, DIM:].bitcast(I32),
-                in_=Wqkv_scales[:, ROWS * quad : ROWS * (quad + 1), DIM:].bitcast(I32),
-            )
+
+        def load_down_bias():
+            for a in range(ADAPTERS):
+                nc.sync.dma_start(out=down_bias[a][:], in_=down_bias_in[a].rearrange("(p t) -> p t", t=PACK))
 
         def load_up_planes(a):
             for quad in range(QUADRANTS):
@@ -162,11 +170,24 @@ def tile_attention_pa_kernel(
                 in_=up_words_in[a].rearrange("g p n t -> p (g n t)").bitcast(I32)[:, cols],
             )
 
+        load_x(0)
+        load_x(1)
+        load_x(2)
+        load_x(3)
+        load_wqkv_scales(0, DIM)
+        load_wqkv(0, N_TILE)
+        load_wqkv(N_TILE, N_TILE)
+        load_down_planes(0)
+        load_down_words(0)
+        load_down_words(1)
+        load_down_planes(1)
+        load_down_bias()
         load_wqkv(DIM, WIDE)
-        load_up_planes(0)
+        load_wqkv_scales(DIM, 3 * DIM)
         load_up_words(0, 0)
-        load_up_planes(1)
+        load_up_planes(0)
         load_up_words(1, 0)
+        load_up_planes(1)
         load_wqkv(DIM + WIDE, WIDE)
         load_up_words(0, 1)
         load_up_words(1, 1)
@@ -227,11 +248,10 @@ def tile_attention_pa_kernel(
                 in_=down_words_given[a][:].bitcast(I32).rearrange("p g (m t) -> p g m t", t=PACK),
             )
             down_words.append(words)
-            if a == 0:
-                nc.vector.tensor_copy(
-                    out=down_planes[:].rearrange("p (t m) -> p m t", t=PACK),
-                    in_=down_planes_given[:].rearrange("p (m t) -> p m t", t=PACK),
-                )
+            nc.vector.tensor_copy(
+                out=down_planes[:, a, :].rearrange("p (t m) -> p m t", t=PACK),
+                in_=down_planes_given[:, a, :].rearrange("p (m t) -> p m t", t=PACK),
+            )
 
         def base_passes(acc, i, first, width, stop):
             cols = slice(first, first + width)
@@ -282,7 +302,7 @@ def tile_attention_pa_kernel(
                     nc.tensor.matmul_mx(
                         out=acc[:],
                         lhsT=down_words[a][:, g, t, :].bitcast(FP8X4),
-                        lhsT_scale=down_planes[ROWS * (a * X_PASSES + g) : P, t * P : (t + 1) * P],
+                        lhsT_scale=down_planes[ROWS * g : P, a, t * P : (t + 1) * P],
                         rhs=x_codes[:, g, :].bitcast(FP8X4),
                         rhs_scale=x_scales[:, g, :],
                         start=(g == 0),

@@ -73,14 +73,16 @@ def tile_attention_pa_kernel(
 
         bias_rows = keep.tile([P, BLOCK], BF16)
         warm = keep.tile([P, 2], F32)
-        wqkv_planes = keep.tile([P, 3 * DIM], U8, align_bytes=64)
+        query_planes = keep.tile([P, X_PASSES, DIM], U8, align_bytes=64)
+        kv_planes = keep.tile([P, X_PASSES, 2 * DIM], U8, align_bytes=64)
         up_planes = keep.tile([P, ADAPTERS, N_TILE], U8, align_bytes=64)
         down_planes_given = keep.tile([P, ADAPTERS, MID], U8, align_bytes=64)
         down_planes = keep.tile([P, ADAPTERS, MID], U8, align_bytes=64)
         ones = keep.tile([P, N_TILE], BF16)
         nc.vector.memset(ones[:], 1.0)
         nc.vector.memset(warm[:], 0.0)
-        nc.vector.memset(wqkv_planes[:].bitcast(I32), 0)
+        nc.vector.memset(query_planes[:].rearrange("p g n -> p (g n)").bitcast(I32), 0)
+        nc.vector.memset(kv_planes[:].rearrange("p g n -> p (g n)").bitcast(I32), 0)
         nc.vector.memset(down_planes_given[:].rearrange("p a n -> p (a n)").bitcast(I32), 0)
         nc.vector.memset(up_planes[:].rearrange("p b n -> p (b n)").bitcast(I32), 0)
 
@@ -97,18 +99,19 @@ def tile_attention_pa_kernel(
         ident = keep.tile([P, P], F32)
         make_identity(nc, ident[:])
 
-        x_sb = []
+        x_tiles = keep.tile([P, TOKEN_TILES, DIM], BF16)
+        x_in = x.rearrange("i p k -> p i k")
 
-        def load_x(i):
-            x_tile = keep.tile([P, DIM], BF16, name="x%d" % i)
-            nc.sync.dma_start(out=x_tile[:], in_=x[i])
-            x_sb.append(x_tile)
+        def load_x(first, last):
+            nc.sync.dma_start(out=x_tiles[:, first:last, :], in_=x_in[:, first:last, :])
 
-        def load_wqkv_scales(first, last):
+        def load_wqkv_scales(planes, first, last):
             for quad in range(QUADRANTS):
                 nc.sync.dma_start(
-                    out=wqkv_planes[32 * quad : 32 * quad + X_PASSES * ROWS, first:last].bitcast(I32),
-                    in_=Wqkv_scales[:, ROWS * quad : ROWS * (quad + 1), first:last].bitcast(I32),
+                    out=planes[32 * quad : 32 * quad + ROWS, :, :].bitcast(I32),
+                    in_=Wqkv_scales[:, ROWS * quad : ROWS * (quad + 1), first:last]
+                    .bitcast(I32)
+                    .rearrange("g r n -> r g n"),
                 )
 
         wqkv = keep.tile([P, X_PASSES, 3 * DIM], U32, align_bytes=64)
@@ -170,11 +173,10 @@ def tile_attention_pa_kernel(
                 in_=up_words_in[a].rearrange("g p n t -> p (g n t)").bitcast(I32)[:, cols],
             )
 
-        load_x(0)
-        load_x(1)
-        load_x(2)
-        load_x(3)
-        load_wqkv_scales(0, DIM)
+        load_x(0, 1)
+        load_x(1, 2)
+        load_x(2, 4)
+        load_wqkv_scales(query_planes, 0, DIM)
         load_wqkv(0, N_TILE)
         load_wqkv(N_TILE, N_TILE)
         load_down_planes(0)
@@ -183,7 +185,7 @@ def tile_attention_pa_kernel(
         load_down_planes(1)
         load_down_bias()
         load_wqkv(DIM, WIDE)
-        load_wqkv_scales(DIM, 3 * DIM)
+        load_wqkv_scales(kv_planes, DIM, 3 * DIM)
         load_up_words(0, 0)
         load_up_planes(0)
         load_up_words(1, 0)
@@ -200,7 +202,7 @@ def tile_attention_pa_kernel(
             nc.tensor.matmul(out=idle[:], lhsT=ones[:, :P], rhs=ones[:], start=True, stop=True)
         for i in range(TOKEN_TILES):
             rows = slice(i * P, (i + 1) * P)
-            x_words = x_sb[i][:].bitcast(F32)
+            x_words = x_tiles[:, i, :].bitcast(F32)
             flipped = psum.tile([P, X_PASSES, PAIRS, P], F32, tag="bank")
             for g in range(X_PASSES):
                 for u in range(PAIRS):
@@ -256,13 +258,14 @@ def tile_attention_pa_kernel(
         def base_passes(acc, i, first, width, stop):
             cols = slice(first, first + width)
             rows = slice(i * P, (i + 1) * P)
+            planes, begin = (query_planes, 0) if first < DIM else (kv_planes, DIM)
             for g in range(X_PASSES):
                 nc.tensor.matmul_mx(
                     out=acc[:],
                     lhsT=x_codes[:, g, rows].bitcast(FP8X4),
                     lhsT_scale=x_scales[:, g, rows],
                     rhs=wqkv[:, g, cols].bitcast(FP8X4),
-                    rhs_scale=wqkv_planes[ROWS * g : P, cols],
+                    rhs_scale=planes[:, g, first - begin : first - begin + width],
                     start=(g == 0),
                     stop=(stop and g == X_PASSES - 1),
                 )

@@ -231,29 +231,18 @@ def tile_attention_pa_kernel(
         kv_bias = keep.tile([P, KV_CHUNKS, N_TILE], F32, align_bytes=64)
         chunk_blocks = N_TILE // BLOCK
 
-        def repeat_bias(spread, chunk):
+        bias_sums = keep.tile([P, BLOCKS], F32)
+
+        def repeat_bias(chunk):
             nc.scalar.copy(
                 out=bias_blocks[:, chunk, :].rearrange("p (b i) -> p b i", i=BLOCK),
-                in_=spread[:, chunk * chunk_blocks : (chunk + 1) * chunk_blocks]
+                in_=bias_sums[:, chunk * chunk_blocks : (chunk + 1) * chunk_blocks]
                 .unsqueeze(2)
                 .to_broadcast([P, chunk_blocks, BLOCK]),
             )
 
         def turn_bias(chunk):
             nc.vector.transpose(out=kv_bias[:, chunk, :], in_=bias_blocks[:, chunk, :])
-
-        down_words = []
-        for a in range(ADAPTERS):
-            words = keep.tile([P, X_PASSES, PACK, P], U32, name="down_words%d" % a, align_bytes=64)
-            nc.vector.tensor_copy(
-                out=words[:].bitcast(I32).rearrange("p g t m -> p g m t"),
-                in_=down_words_given[a][:].bitcast(I32).rearrange("p g (m t) -> p g m t", t=PACK),
-            )
-            down_words.append(words)
-            nc.vector.tensor_copy(
-                out=down_planes[:, a, :].rearrange("p (t m) -> p m t", t=PACK),
-                in_=down_planes_given[:, a, :].rearrange("p (m t) -> p m t", t=PACK),
-            )
 
         def base_passes(acc, i, first, width, stop):
             cols = slice(first, first + width)
@@ -270,8 +259,23 @@ def tile_attention_pa_kernel(
                     stop=(stop and g == X_PASSES - 1),
                 )
 
+        down_words = []
+        for a in range(ADAPTERS):
+            words = keep.tile([P, X_PASSES, PACK, P], U32, name="down_words%d" % a, align_bytes=64)
+            down_words.append(words)
+
+        def move_down_weights(a):
+            nc.vector.tensor_copy(
+                out=down_planes[:, a, :].rearrange("p (t m) -> p m t", t=PACK),
+                in_=down_planes_given[:, a, :].rearrange("p (m t) -> p m t", t=PACK),
+            )
+            given = down_words_given[a][:].bitcast(I32).rearrange("p g (m t) -> p g t m", t=PACK)
+            for t in range(PACK):
+                nc.vector.tensor_copy(out=down_words[a][:, :, t, :].bitcast(I32), in_=given[:, :, t, :])
+
         results = {}
-        for chunk in range(Q_CHUNKS):
+
+        def query_chunk(chunk):
             cols = slice(chunk * N_TILE, (chunk + 1) * N_TILE)
             for i in range(TOKEN_TILES):
                 acc = psum.tile([P, N_TILE], F32, tag="bank")
@@ -279,21 +283,26 @@ def tile_attention_pa_kernel(
                 if chunk == 0:
                     result = stage.tile([P, WIDE], F32, tag="result")
                     results[i] = result
-                    nc.scalar.copy(out=results[i][:, cols], in_=acc[:])
-                else:
+                if chunk == 1 and i >= 2:
                     nc.vector.tensor_copy(out=results[i][:, cols], in_=acc[:])
+                else:
+                    nc.scalar.copy(out=results[i][:, cols], in_=acc[:])
+                if chunk == 1:
                     nc.sync.dma_start(out=out[i, :, :WIDE], in_=results[i][:])
-            if chunk == 0:
-                spread = psum.tile([P, BLOCKS], F32, tag="bank")
-                nc.tensor.matmul(
-                    out=spread[:],
-                    lhsT=bias_cols[:].rearrange("p r j -> p (r j)"),
-                    rhs=fold[:],
-                    start=True,
-                    stop=True,
-                )
-                for kv_chunk in range(KV_CHUNKS):
-                    repeat_bias(spread, kv_chunk)
+
+        query_chunk(0)
+        spread = psum.tile([P, BLOCKS], F32, tag="bank")
+        nc.tensor.matmul(
+            out=spread[:],
+            lhsT=bias_cols[:].rearrange("p r j -> p (r j)"),
+            rhs=fold[:],
+            start=True,
+            stop=True,
+        )
+        nc.scalar.copy(out=bias_sums[:], in_=spread[:])
+        move_down_weights(0)
+        query_chunk(1)
+        move_down_weights(1)
 
         hidden = []
         for a in range(ADAPTERS):
@@ -347,6 +356,8 @@ def tile_attention_pa_kernel(
                 group_hidden(1, tile_rows[i + 1])
             quantise_hidden(1, tile_rows[i])
 
+        for chunk in range(KV_CHUNKS):
+            repeat_bias(chunk)
         for chunk in range(KV_CHUNKS // 2):
             turn_bias(chunk)
 

@@ -177,7 +177,8 @@ def tile_attention_pa_kernel(
         load_x(1, 2)
         load_x(2, 4)
         load_wqkv_scales(query_planes, 0, DIM)
-        load_wqkv(0, N_TILE)
+        load_wqkv_pass(0, 0, N_TILE)
+        load_wqkv_pass(1, 0, N_TILE)
         load_wqkv(N_TILE, N_TILE)
         load_down_planes(0)
         load_down_words(0)

from contextlib import ExitStack

import concourse.mybir as mybir
from concourse.masks import make_identity

F32 = mybir.dt.float32
BF16 = mybir.dt.bfloat16
I32 = mybir.dt.int32
U32 = mybir.dt.uint32
U8 = mybir.dt.uint8
FP8X4 = mybir.dt.float8_e4m3fn_x4
ADD = mybir.AluOpType.add
TANH = mybir.ActivationFunctionType.Tanh

P = 128
PACK = 4
PAIRS = 2
K_PASS = P * PACK
N_TILE = 512
TOKEN_TILES = 4
TOKENS = TOKEN_TILES * P
DIM = 1024
MID = 512
X_PASSES = DIM // K_PASS
ADAPTERS = 2
Q_CHUNKS = DIM // N_TILE
KV_CHUNKS = 2 * DIM // N_TILE
WIDE = 2 * N_TILE
KV_HALVES = 2 * DIM // WIDE
QUADRANTS = 4
ROWS = 4
UP_COLS = 2 * DIM
BLOCK = 32
BLOCKS = UP_COLS // BLOCK
WARM_UP = 6

FLOPS = 2 * TOKENS * (DIM * 3 * DIM + ADAPTERS * (DIM * MID + MID * 2 * DIM))


def tile_attention_pa_kernel(
    tc,
    x,
    Wqkv_words,
    Wqkv_scales,
    down_w_words,
    down_w_scales,
    down_b,
    up_w_words,
    up_w_scales,
    up_b,
    pdown_w_words,
    pdown_w_scales,
    pdown_b,
    pup_w_words,
    pup_w_scales,
    pup_b,
    out,
):
    nc = tc.nc
    down_words_in = (pdown_w_words, down_w_words)
    down_scales_in = (pdown_w_scales, down_w_scales)
    down_bias_in = (pdown_b, down_b)
    up_words_in = (pup_w_words, up_w_words)
    up_scales_in = (pup_w_scales, up_w_scales)
    up_bias_in = (pup_b, up_b)

    with ExitStack() as ctx:
        ctx.enter_context(tc.manual_schedule())
        keep = ctx.enter_context(tc.tile_pool(name="keep", bufs=1))
        work = ctx.enter_context(tc.tile_pool(name="work", bufs=4))
        stage = ctx.enter_context(tc.tile_pool(name="stage", bufs=12))
        psum = ctx.enter_context(tc.psum_pool(name="psum", bufs=8))

        bias_rows = keep.tile([P, BLOCK], BF16)
        warm = keep.tile([P, 2], F32)
        query_planes = keep.tile([P, X_PASSES, DIM], U8, align_bytes=64)
        kv_planes = keep.tile([P, X_PASSES, 2 * DIM], U8, align_bytes=64)
        up_planes = keep.tile([P, ADAPTERS, N_TILE], U8, align_bytes=64)
        down_planes_given = keep.tile([P, ADAPTERS, MID], U8, align_bytes=64)
        down_planes = keep.tile([P, ADAPTERS, MID], U8, align_bytes=64)
        ones = keep.tile([P, N_TILE], BF16)
        nc.vector.memset(ones[:], 1.0)
        nc.vector.memset(warm[:], 0.0)
        nc.vector.memset(query_planes[:].rearrange("p g n -> p (g n)").bitcast(I32), 0)
        nc.vector.memset(kv_planes[:].rearrange("p g n -> p (g n)").bitcast(I32), 0)
        nc.vector.memset(down_planes_given[:].rearrange("p a n -> p (a n)").bitcast(I32), 0)
        nc.vector.memset(up_planes[:].rearrange("p b n -> p (b n)").bitcast(I32), 0)

        def load_up_bias():
            for a in range(ADAPTERS):
                nc.scalar.dma_start(
                    out=bias_rows[a * BLOCKS : (a + 1) * BLOCKS, :],
                    in_=up_bias_in[a].rearrange("(b j) -> b j", j=BLOCK),
                )

        load_up_bias()
        nc.scalar.activation(out=warm[:, 1:2], in_=warm[:, 0:1], func=TANH)

        ident = keep.tile([P, P], F32)
        make_identity(nc, ident[:])

        x_tiles = keep.tile([P, TOKEN_TILES, DIM], BF16)
        x_in = x.rearrange("i p k -> p i k")

        def load_x(first, last):
            nc.sync.dma_start(out=x_tiles[:, first:last, :], in_=x_in[:, first:last, :])

        def load_wqkv_scales(planes, first, last):
            for quad in range(QUADRANTS):
                nc.sync.dma_start(
                    out=planes[32 * quad : 32 * quad + ROWS, :, :].bitcast(I32),
                    in_=Wqkv_scales[:, ROWS * quad : ROWS * (quad + 1), first:last]
                    .bitcast(I32)
                    .rearrange("g r n -> r g n"),
                )

        wqkv = keep.tile([P, X_PASSES, 3 * DIM], U32, align_bytes=64)
        wqkv_in = Wqkv_words.rearrange("g p n t -> p g (n t)").bitcast(I32)

        def load_wqkv(first, width):
            cols = slice(first, first + width)
            nc.sync.dma_start(out=wqkv[:, :, cols].bitcast(I32), in_=wqkv_in[:, :, cols])

        def load_wqkv_pass(g, first, width):
            cols = slice(first, first + width)
            nc.sync.dma_start(out=wqkv[:, g, cols].bitcast(I32), in_=wqkv_in[:, g, cols])

        down_words_given = []
        for a in range(ADAPTERS):
            words = keep.tile([P, X_PASSES, MID], U32, name="down_words_given%d" % a, align_bytes=64)
            down_words_given.append(words)

        def load_down_planes(a):
            for quad in range(QUADRANTS):
                nc.sync.dma_start(
                    out=down_planes_given[32 * quad : 32 * quad + X_PASSES * ROWS, a, :].bitcast(I32),
                    in_=down_scales_in[a][:, ROWS * quad : ROWS * (quad + 1), :].bitcast(I32),
                )

        def load_down_words(a):
            nc.sync.dma_start(
                out=down_words_given[a][:].bitcast(I32),
                in_=down_words_in[a].rearrange("g p n t -> p g (n t)").bitcast(I32),
            )

        down_bias = []
        for a in range(ADAPTERS):
            bias_tile = keep.tile([P, PACK], BF16, name="down_bias%d" % a)
            down_bias.append(bias_tile)

        def load_down_bias():
            for a in range(ADAPTERS):
                nc.sync.dma_start(out=down_bias[a][:], in_=down_bias_in[a].rearrange("(p t) -> p t", t=PACK))

        def load_up_planes(a):
            for quad in range(QUADRANTS):
                nc.sync.dma_start(
                    out=up_planes[32 * quad : 32 * quad + KV_CHUNKS * ROWS, a, :].bitcast(I32),
                    in_=up_scales_in[a][0, ROWS * quad : ROWS * (quad + 1), :]
                    .bitcast(I32)
                    .rearrange("r (c n) -> c r n", c=KV_CHUNKS),
                )

        up_words = []
        for a in range(ADAPTERS):
            words = keep.tile([P, UP_COLS], U32, name="up_words%d" % a, align_bytes=64)
            up_words.append(words)

        def load_up_words(a, part):
            cols = slice(part * WIDE, (part + 1) * WIDE)
            nc.sync.dma_start(
                out=up_words[a][:, cols].bitcast(I32),
                in_=up_words_in[a].rearrange("g p n t -> p (g n t)").bitcast(I32)[:, cols],
            )

        load_x(0, 1)
        load_x(1, 2)
        load_x(2, 4)
        load_wqkv_scales(query_planes, 0, DIM)
        load_wqkv_pass(0, 0, N_TILE)
        load_wqkv_pass(1, 0, N_TILE)
        load_wqkv(N_TILE, N_TILE)
        load_down_planes(0)
        load_down_words(0)
        load_down_words(1)
        load_down_planes(1)
        load_down_bias()
        load_wqkv(DIM, WIDE)
        load_wqkv_scales(kv_planes, DIM, 3 * DIM)
        load_up_words(0, 0)
        load_up_planes(0)
        load_up_words(1, 0)
        load_up_planes(1)
        load_wqkv(DIM + WIDE, WIDE)
        load_up_words(0, 1)
        load_up_words(1, 1)

        x_codes = keep.tile([P, X_PASSES, TOKENS], U32, align_bytes=64)
        x_scales = keep.tile([P, X_PASSES, TOKENS], U8, align_bytes=64)
        half = K_PASS // 2
        idle = psum.tile([P, N_TILE], F32, tag="bank")
        for n in range(WARM_UP):
            nc.tensor.matmul(out=idle[:], lhsT=ones[:, :P], rhs=ones[:], start=True, stop=True)
        for i in range(TOKEN_TILES):
            rows = slice(i * P, (i + 1) * P)
            x_words = x_tiles[:, i, :].bitcast(F32)
            flipped = psum.tile([P, X_PASSES, PAIRS, P], F32, tag="bank")
            for g in range(X_PASSES):
                for u in range(PAIRS):
                    nc.tensor.transpose(
                        flipped[:, g, u, :], x_words[:, g * half + u : (g + 1) * half : PAIRS], ident[:]
                    )
            if i == TOKEN_TILES // 2 - 1:
                for n in range(2):
                    nc.tensor.matmul(out=idle[:], lhsT=ones[:, :P], rhs=ones[:], start=True, stop=True)
            grouped = work.tile([P, X_PASSES, P, PACK], BF16, tag="grouped", align_bytes=64)
            nc.scalar.copy(out=grouped[:].bitcast(F32), in_=flipped[:].rearrange("p g u r -> p g r u"))
            for g in range(X_PASSES):
                nc.vector.quantize_mx(
                    out=x_codes[:, g, rows].bitcast(FP8X4),
                    scales=x_scales[:, g, rows],
                    in_=grouped[:, g, :, :].rearrange("p r t -> p (r t)"),
                )

        fold = keep.tile([P, BLOCKS], BF16)
        nc.vector.tensor_tensor(out=fold[:], in0=ident[:, :BLOCKS], in1=ident[:, BLOCKS:], op=ADD)
        bias_cols = keep.tile([P, QUADRANTS, BLOCK], BF16)
        nc.vector.tensor_copy(
            out=bias_cols[:], in_=bias_rows[:].unsqueeze(1).to_broadcast([P, QUADRANTS, BLOCK])
        )
        bias_blocks = keep.tile([P, KV_CHUNKS, N_TILE], F32, align_bytes=64)
        kv_bias = keep.tile([P, KV_CHUNKS, N_TILE], F32, align_bytes=64)
        chunk_blocks = N_TILE // BLOCK

        bias_sums = keep.tile([P, BLOCKS], F32)

        def repeat_bias(chunk):
            nc.scalar.copy(
                out=bias_blocks[:, chunk, :].rearrange("p (b i) -> p b i", i=BLOCK),
                in_=bias_sums[:, chunk * chunk_blocks : (chunk + 1) * chunk_blocks]
                .unsqueeze(2)
                .to_broadcast([P, chunk_blocks, BLOCK]),
            )

        def turn_bias(chunk):
            nc.vector.transpose(out=kv_bias[:, chunk, :], in_=bias_blocks[:, chunk, :])

        def base_passes(acc, i, first, width, stop):
            cols = slice(first, first + width)
            rows = slice(i * P, (i + 1) * P)
            planes, begin = (query_planes, 0) if first < DIM else (kv_planes, DIM)
            for g in range(X_PASSES):
                nc.tensor.matmul_mx(
                    out=acc[:],
                    lhsT=x_codes[:, g, rows].bitcast(FP8X4),
                    lhsT_scale=x_scales[:, g, rows],
                    rhs=wqkv[:, g, cols].bitcast(FP8X4),
                    rhs_scale=planes[:, g, first - begin : first - begin + width],
                    start=(g == 0),
                    stop=(stop and g == X_PASSES - 1),
                )

        down_words = []
        for a in range(ADAPTERS):
            words = keep.tile([P, X_PASSES, PACK, P], U32, name="down_words%d" % a, align_bytes=64)
            down_words.append(words)

        def move_down_weights(a):
            nc.vector.tensor_copy(
                out=down_planes[:, a, :].rearrange("p (t m) -> p m t", t=PACK),
                in_=down_planes_given[:, a, :].rearrange("p (m t) -> p m t", t=PACK),
            )
            given = down_words_given[a][:].bitcast(I32).rearrange("p g (m t) -> p g t m", t=PACK)
            for t in range(PACK):
                nc.vector.tensor_copy(out=down_words[a][:, :, t, :].bitcast(I32), in_=given[:, :, t, :])

        results = {}

        def query_chunk(chunk):
            cols = slice(chunk * N_TILE, (chunk + 1) * N_TILE)
            for i in range(TOKEN_TILES):
                acc = psum.tile([P, N_TILE], F32, tag="bank")
                base_passes(acc, i, chunk * N_TILE, N_TILE, stop=True)
                if chunk == 0:
                    result = stage.tile([P, WIDE], F32, tag="result")
                    results[i] = result
                if chunk == 1 and i >= 2:
                    nc.vector.tensor_copy(out=results[i][:, cols], in_=acc[:])
                else:
                    nc.scalar.copy(out=results[i][:, cols], in_=acc[:])
                if chunk == 1:
                    nc.sync.dma_start(out=out[i, :, :WIDE], in_=results[i][:])

        query_chunk(0)
        spread = psum.tile([P, BLOCKS], F32, tag="bank")
        nc.tensor.matmul(
            out=spread[:],
            lhsT=bias_cols[:].rearrange("p r j -> p (r j)"),
            rhs=fold[:],
            start=True,
            stop=True,
        )
        nc.scalar.copy(out=bias_sums[:], in_=spread[:])
        move_down_weights(0)
        query_chunk(1)
        move_down_weights(1)

        hidden = []
        for a in range(ADAPTERS):
            hidden_tile = keep.tile([P, PACK, TOKENS], BF16, name="hidden%d" % a)
            hidden.append(hidden_tile)
            for t in range(PACK):
                acc = psum.tile([P, TOKENS], F32, tag="bank")
                for g in range(X_PASSES):
                    nc.tensor.matmul_mx(
                        out=acc[:],
                        lhsT=down_words[a][:, g, t, :].bitcast(FP8X4),
                        lhsT_scale=down_planes[ROWS * g : P, a, t * P : (t + 1) * P],
                        rhs=x_codes[:, g, :].bitcast(FP8X4),
                        rhs_scale=x_scales[:, g, :],
                        start=(g == 0),
                        stop=(g == X_PASSES - 1),
                    )
                nc.scalar.activation(
                    out=hidden_tile[:, t, :], in_=acc[:], func=TANH, bias=down_bias[a][:, t : t + 1]
                )

        h_grouped = []
        h_codes = []
        h_scales = []
        for a in range(ADAPTERS):
            grouped_tile = keep.tile([P, TOKENS, PACK], BF16, name="h_grouped%d" % a, align_bytes=64)
            codes_tile = keep.tile([P, TOKENS], U32, name="h_codes%d" % a, align_bytes=64)
            scales_tile = keep.tile([P, TOKENS], U8, name="h_scales%d" % a, align_bytes=64)
            h_grouped.append(grouped_tile)
            h_codes.append(codes_tile)
            h_scales.append(scales_tile)

        def group_hidden(a, rows):
            nc.vector.tensor_copy(
                out=h_grouped[a][:, rows, :], in_=hidden[a][:, :, rows].rearrange("p t r -> p r t")
            )

        def quantise_hidden(a, rows):
            nc.vector.quantize_mx(
                out=h_codes[a][:, rows].bitcast(FP8X4),
                scales=h_scales[a][:, rows],
                in_=h_grouped[a][:, rows, :].rearrange("p r t -> p (r t)"),
            )

        group_hidden(0, slice(0, TOKENS))
        quantise_hidden(0, slice(0, TOKENS))
        tile_rows = [slice(i * P, (i + 1) * P) for i in range(TOKEN_TILES)]
        group_hidden(1, tile_rows[0])
        for i in range(TOKEN_TILES):
            if i + 1 < TOKEN_TILES:
                group_hidden(1, tile_rows[i + 1])
            quantise_hidden(1, tile_rows[i])

        for chunk in range(KV_CHUNKS):
            repeat_bias(chunk)
        for chunk in range(KV_CHUNKS // 2):
            turn_bias(chunk)

        pieces = []
        for part in range(KV_HALVES):
            for i in range(TOKEN_TILES):
                last = part == KV_HALVES - 1 and i == TOKEN_TILES - 1
                widths = [N_TILE, N_TILE // 2, N_TILE // 2] if last else [N_TILE, N_TILE]
                first = part * WIDE
                for width in widths:
                    first += width
                    whole = first == (part + 1) * WIDE
                    stored = width if last else (WIDE if whole else 0)
                    pieces.append((i, first - width, width, stored))

        def kv_open(piece):
            i, first, width, stored = piece
            acc = psum.tile([P, width], F32, tag="bank")
            base_passes(acc, i, DIM + first, width, stop=False)
            return acc

        def kv_close(acc, piece):
            i, first, width, stored = piece
            chunk = first // N_TILE
            offset = first % N_TILE
            for a in range(ADAPTERS):
                nc.tensor.matmul_mx(
                    out=acc[:],
                    lhsT=h_codes[a][:, tile_rows[i]].bitcast(FP8X4),
                    lhsT_scale=h_scales[a][:, tile_rows[i]],
                    rhs=up_words[a][:, first : first + width].bitcast(FP8X4),
                    rhs_scale=up_planes[ROWS * chunk : P, a, offset : offset + width],
                    start=False,
                    stop=(a == ADAPTERS - 1),
                )
            if first % WIDE == 0:
                result = stage.tile([P, WIDE], F32, tag="result")
                results[i] = result
            place = first % WIDE
            nc.vector.tensor_tensor(
                out=results[i][:, place : place + width],
                in0=acc[:],
                in1=kv_bias[:, chunk, offset : offset + width],
                op=ADD,
            )
            if stored:
                end = first + width
                nc.sync.dma_start(
                    out=out[i, :, DIM + end - stored : DIM + end],
                    in_=results[i][:, place + width - stored : place + width],
                )

        AHEAD = 7
        opened = [kv_open(piece) for piece in pieces[:AHEAD]]
        for n in range(AHEAD):
            kv_close(opened[n], pieces[n])
            if n % 2 == 1 and n < KV_CHUNKS:
                turn_bias(KV_CHUNKS // 2 + n // 2)
        for piece in pieces[AHEAD:]:
            kv_close(kv_open(piece), piece)
